import numpy as np
import ml_dtypes


def mxq(x, axis, fmt="e4m3"):
    dtype, down = {"e4m3": (ml_dtypes.float8_e4m3fn, 7), "e5m2": (ml_dtypes.float8_e5m2, 14)}[fmt]
    v = np.moveaxis(np.asarray(x, np.float32).astype(ml_dtypes.bfloat16).astype(np.float64), axis, -1)
    blocks = v.reshape(v.shape[:-1] + (-1, 32))
    amax = np.abs(blocks).max(-1, keepdims=True)
    byte = np.maximum(np.where(amax > 0, np.frexp(amax)[1] - 1 + 127, 0) - down, 1)
    scale = np.exp2(byte - 127.0)
    codes = (blocks / scale).astype(np.float32).astype(dtype).astype(np.float64)
    return np.moveaxis((codes * scale).reshape(v.shape), -1, axis)


WIDE = False


def mx_kscale(k):
    if not WIDE:
        return np.ones(k)
    levels = np.array([18, -18])
    if k % 512:
        return np.exp2(np.random.permutation(np.resize(levels, k // 32))).repeat(32)
    a = np.empty((k // 512, 16))
    for p in range(k // 512):
        a[p, :8] = np.random.permutation(np.resize(levels, 8))
        for g in range(8):
            far = levels[np.abs(levels - a[p, g]) >= 10]
            a[p, g + 8] = far[np.random.randint(len(far))]
    return np.exp2(a.ravel()).repeat(32)


BF16 = ml_dtypes.bfloat16


def bf(x):
    return np.asarray(x, np.float32).astype(BF16)


def f64(x):
    return np.asarray(x).astype(np.float64)


B, D_IN, HID, OUT = 1024, 512, 2048, 1024


def setup_inputs():
    s = mx_kscale(B)[:, None]
    u = mx_kscale(OUT)
    v = mx_kscale(HID)
    vc = np.concatenate([np.ones(D_IN), v])
    x0 = bf(np.random.standard_normal((B, D_IN)))
    W1_0 = bf(np.random.standard_normal((HID, D_IN)) / np.sqrt(D_IN))
    b1 = bf(np.random.standard_normal(HID) * 0.3)
    W2_0 = bf(np.random.standard_normal((OUT, D_IN + HID)) / np.sqrt(D_IN + HID))
    b2 = bf(np.random.standard_normal(OUT) * 0.3)
    while True:
        z1 = f64(x0) @ f64(W1_0).T + f64(b1)
        near = np.abs(z1).min(axis=1) < 1e-5
        if not near.any():
            break
        x0[near] = bf(np.random.standard_normal((np.count_nonzero(near), D_IN)))
    g = bf(np.random.standard_normal((B, OUT)) * np.exp2(np.random.randint(-6, 1, (B, 1))) * 4.0 / s * u)
    return {"x": bf(f64(x0) * s),
            "W1": bf(f64(W1_0) / v[:, None]),
            "b1": b1,
            "W2": bf(f64(W2_0) * vc[None, :] / u[:, None]),
            "b2": b2,
            "z1": np.asarray(z1, np.float32),
            "grad_out": g}


def reference(x, W1, b1, W2, b2, z1, grad_out):
    dc = mxq(f64(grad_out), 1, "e5m2") @ mxq(f64(W2), 0, "e4m3")
    dz1 = dc[:, D_IN:] * (f64(z1) > 0.0)
    dx = dc[:, :D_IN] + (mxq(dz1, 1, "e5m2") @ mxq(f64(W1), 0, "e4m3"))
    dW1 = mxq(dz1, 0, "e5m2").T @ mxq(f64(x), 0, "e4m3")
    return dx, dW1

@@ -1,0 +1,436 @@
+from contextlib import ExitStack
+
+import concourse.mybir as mybir
+from concourse.masks import make_identity
+
+B, D_IN, HID, OUT = 1024, 512, 2048, 1024
+
+FLOPS = 2 * B * OUT * (D_IN + HID) + 2 * (2 * B * HID * D_IN)
+BYTES = 2 * (B * D_IN + HID * D_IN + OUT * (D_IN + HID) + B * OUT) + 4 * B * HID + 4 * (B * D_IN + HID * D_IN)
+
+F32 = mybir.dt.float32
+BF16 = mybir.dt.bfloat16
+U32 = mybir.dt.uint32
+U8 = mybir.dt.uint8
+E4M3 = mybir.dt.float8_e4m3fn_x4
+E5M2 = mybir.dt.float8_e5m2_x4
+IS_GT = mybir.AluOpType.is_gt
+MULT = mybir.AluOpType.mult
+ADD = mybir.AluOpType.add
+
+P = 128
+PACK = 4
+W = 512
+N_G = B // W
+N_H = HID // W
+N_P = OUT // W
+
+
+def tile_dpn_v_kernel(tc, x, W1, b1, W2, b2, z1, grad_out, out_0, out_1):
+    nc = tc.nc
+
+    with ExitStack() as ctx:
+
+        def pool(name, bufs):
+            return ctx.enter_context(tc.tile_pool(name=name, bufs=bufs))
+
+        const = pool("const", 1)
+        graw_pool = pool("graw_pool", 2)
+        raw_pool = pool("raw_pool", 6)
+        z_pool = pool("z_pool", 4)
+        dz_pool = pool("dz_pool", 3)
+        grp_pool = pool("grp_pool", 5)
+        grpa_pool = pool("grpa_pool", 2)
+        grpb_pool = pool("grpb_pool", 3)
+        keep = pool("keep", 1)
+        w2_pool = pool("w2_pool", 6)
+        a_pool = pool("a_pool", 5)
+        b_pool = pool("b_pool", 8)
+        out_pool = pool("out_pool", 2)
+        out0_pool = pool("out0_pool", 2)
+        ps_dc = ctx.enter_context(tc.psum_pool(name="ps_dc", bufs=3))
+        ps_tr = ctx.enter_context(tc.psum_pool(name="ps_tr", bufs=2))
+        ps_out = ctx.enter_context(tc.psum_pool(name="ps_out", bufs=3))
+
+        ident = const.tile([P, P], F32, name="ident", align_bytes=64)
+        make_identity(nc, ident[:])
+
+        ctx.enter_context(tc.manual_schedule())
+
+        g_rows = grad_out.rearrange("(g p j) w -> g p j w", g=N_G, j=PACK)
+        z_rows = z1.rearrange("(g p j) h -> g p j h", g=N_G, j=PACK)
+        x_rows = x.rearrange("(g p j) d -> g p j d", g=N_G, j=PACK)
+        w2_rows = W2.rearrange("(g p j) c -> g p j c", g=N_P, j=PACK)
+        w1_rows = W1.rearrange("(g p j) d -> g p j d", g=N_H, j=PACK)
+        out0_rows = out_0.rearrange("(g p j) d -> g p j d", g=N_G, j=PACK)
+        out1_rows = out_1.rearrange("(h q c) d -> h q c d", h=N_H, c=PACK)
+
+        raws = {}
+        groups = {}
+        codes = {}
+        banks = {}
+
+        queues = {"load": [], "pe": [], "v": [], "s": [], "store": []}
+
+        def put(queue, name, needs, fn, *args):
+            queues[queue].append((name, needs, fn, args))
+
+        def load_g(grp, jp):
+            if jp == 0:
+                raws["g", grp] = graw_pool.tile([P, PACK, OUT], BF16, name="graw", align_bytes=64)
+            t = raws["g", grp]
+            nc.sync.dma_start(out=t[:, 2 * jp : 2 * jp + 2, :], in_=g_rows[grp, :, 2 * jp : 2 * jp + 2, :])
+
+        def load_z(grp, h):
+            t = z_pool.tile([P, PACK, W], F32, name="zt", align_bytes=64)
+            nc.sync.dma_start(out=t[:], in_=z_rows[grp, :, :, h * W : (h + 1) * W])
+            raws["z", grp, h] = t
+
+        def load_w(what):
+            if what[0] == "w2":
+                src = w2_rows[what[2], :, :, D_IN + what[1] * W : D_IN + (what[1] + 1) * W]
+            elif what[0] == "w2x":
+                src = w2_rows[what[1], :, :, 0:D_IN]
+            elif what[0] == "w1":
+                src = w1_rows[what[1]]
+            else:
+                src = x_rows[what[1]]
+            t = raw_pool.tile([P, PACK, W], BF16, name="raw", align_bytes=64)
+            nc.sync.dma_start(out=t[:], in_=src)
+            raws[what] = t
+
+        def new_codes(key):
+            src, tag = keep, "_".join([str(v) for v in key])
+            if key[0] in ("w2", "a", "b"):
+                src, tag = {"w2": (w2_pool, "w2"), "a": (a_pool, "a"), "b": (b_pool, "b")}[key[0]]
+            c = src.tile([P, W], U32, name="c_" + tag, align_bytes=64)
+            s = src.tile([P, W], U8, name="s_" + tag, align_bytes=64)
+            codes[key] = (c, s)
+
+        def quantize(key, fmt, part=0, parts=1):
+            if part == 0:
+                new_codes(key)
+            c, s = codes[key]
+            cols = slice(part * (W // parts), (part + 1) * (W // parts))
+            wide = slice(part * (PACK * W // parts), (part + 1) * (PACK * W // parts))
+            nc.vector.quantize_mx(
+                out=c[:, cols].bitcast(fmt), scales=s[:, cols], in_=groups[key][:].rearrange("p w k -> p (w k)")[:, wide]
+            )
+
+        def copy(engine, out, in_):
+            if engine == "s":
+                nc.scalar.copy(out=out, in_=in_)
+            else:
+                nc.vector.tensor_copy(out=out, in_=in_)
+
+        def interleave(what, engine):
+            raw = raws[what]
+            grp = grp_pool.tile([P, W, PACK], BF16, name="grp", align_bytes=64)
+            if what[0] == "w2":
+                dst = grp[:].rearrange("p (u q e) k -> p u q e k", u=2, e=2)
+                src = raw[:].rearrange("p k (q u e) -> p u q e k", u=2, e=2)
+            else:
+                dst = grp[:]
+                src = raw[:].rearrange("p k w -> p w k")
+            copy(engine, dst, src)
+            groups[what] = grp
+
+        def transpose_bank(key, w, starts, step):
+            bank = ps_tr.tile([P, 2, 256], F32, name="trb")
+            for u in range(2):
+                for jj in range(2):
+                    o = starts[jj] + u * (1 if step == 2 else P)
+                    nc.tensor.transpose(bank[:, u, jj * P : (jj + 1) * P], w[:, o : o + step * (P - 1) + 1 : step], ident[:])
+            banks[key] = bank
+
+        def g_transpose(grp, pas, jp):
+            w = raws["g", grp][:].rearrange("p j w -> p (j w)").bitcast(F32)
+            transpose_bank(("g", grp, pas, jp), w, [(2 * jp + jj) * (OUT // 2) + pas * (W // 2) for jj in range(2)], 2)
+
+        def b_transpose(grp, h, jp):
+            w = groups["dz", grp, h][:].rearrange("p t w -> p (t w)").bitcast(F32)
+            transpose_bank(("b", grp, h, jp), w, [(2 * jp + jj) * (W // 2) for jj in range(2)], 1)
+
+        def copy_transposed(key, jp, engine):
+            if jp == 0:
+                groups[key] = grpb_pool.tile([P, W, PACK], BF16, name="gb", align_bytes=64)
+            dst = groups[key][:].rearrange("p r k -> p (r k)").bitcast(F32)[:, jp * W : (jp + 1) * W]
+            copy(engine, dst.rearrange("p (r u) -> p r u", u=2), banks[key + (jp,)][:].rearrange("p u r -> p r u"))
+
+        def mx(bank, lhs, t, rhs, start, stop):
+            lc, ls = codes[lhs]
+            rc, rs = codes[rhs]
+            cols = slice(t * P, (t + 1) * P)
+            nc.tensor.matmul_mx(
+                out=bank[:],
+                lhsT=lc[:, cols].bitcast(E5M2),
+                lhsT_scale=ls[:, cols],
+                rhs=rc[:].bitcast(E4M3),
+                rhs_scale=rs[:],
+                start=start,
+                stop=stop,
+            )
+
+        def dc(grp, h, t):
+            bank = ps_dc.tile([P, W], F32, name="dcb")
+            for pas in range(N_P):
+                mx(bank, ("g", grp, pas), t, ("w2", h, pas), pas == 0, pas == N_P - 1)
+            banks["dc", grp, h, t] = bank
+
+        def mask(grp, h, t):
+            if t == 0:
+                groups["dz", grp, h] = dz_pool.tile([P, PACK, W], BF16, name="dz", align_bytes=64)
+            dz = groups["dz", grp, h]
+            bank = banks["dc", grp, h, t]
+            zv = raws["z", grp, h][:, t, :].rearrange("p (q u e) -> p u q e", u=2, e=2)
+            for u in range(2):
+                half = slice(u * 256, (u + 1) * 256)
+                nc.vector.scalar_tensor_tensor(
+                    out=dz[:, t, half].rearrange("p (q e) -> p q e", e=2),
+                    in0=zv[:, u],
+                    scalar=0.0,
+                    in1=bank[:, half].rearrange("p (q e) -> p q e", e=2),
+                    op0=IS_GT,
+                    op1=MULT,
+                )
+
+        def int_a(grp, h):
+            ga = grpa_pool.tile([P, W, PACK], BF16, name="ga", align_bytes=64)
+            nc.vector.tensor_copy(
+                out=ga[:].rearrange("p (u e q) t -> p u e q t", u=2, e=2),
+                in_=groups["dz", grp, h][:].rearrange("p t (u q e) -> p u e q t", u=2, e=2),
+            )
+            groups["a", grp, h] = ga
+
+        outs = {}
+
+        def product(key, terms, t, last_pool):
+            bank = last_pool.tile([P, W], F32, name="dcb" if last_pool is ps_dc else "ob")
+            for i, (lhs, rhs) in enumerate(terms):
+                mx(bank, lhs, t, rhs, i == 0, i == len(terms) - 1)
+            banks[key] = bank
+
+        def out_tile(key):
+            if key not in outs:
+                outs[key] = (out_pool if key[0] == "o1" else out0_pool).tile([P, PACK, D_IN], F32, name=key[0], align_bytes=64)
+            return outs[key]
+
+        def evac(key, t, engine):
+            copy(engine, out_tile(key[:2])[:, t, :], banks[key][:])
+
+        def evac_add(key, t):
+            o = out_tile(key[:2])[:, t, :]
+            nc.vector.tensor_tensor(out=o, in0=banks[key][:], in1=o, op=ADD)
+
+        def store(key, t, n):
+            rows = out1_rows if key[0] == "o1" else out0_rows
+            nc.sync.dma_start(out=rows[key[1], :, t : t + n, :], in_=outs[key][:, t : t + n, :])
+
+        def out0_terms(grp, parts):
+            r = []
+            for part in parts:
+                if part == "x":
+                    r.extend([(("g", grp, pas), ("w2x", pas)) for pas in range(N_P)])
+                else:
+                    r.append((("b", grp, part), ("w1", part)))
+            return r
+
+
+        MODES = {(grp, t): [["x", 0, 1], [2, 3]] for grp in range(2) for t in range(4)}
+        units = [(k % 2, k // 2) for k in range(2 * N_H)]
+
+        def L(what, needs=()):
+            if what[0] == "g":
+                put("load", ("raw",) + what, needs, load_g, what[1], what[2])
+            elif what[0] == "z":
+                put("load", ("raw",) + what, needs, load_z, what[1], what[2])
+            else:
+                put("load", ("raw",) + what, needs, load_w, what)
+
+        def V_int(what):
+            put("v", ("int",) + what, [("raw",) + what], interleave, what, "v")
+
+        def S_int(what):
+            put("s", ("int",) + what, [("raw",) + what], interleave, what, "s")
+
+        def V_q(what):
+            put("v", ("q",) + what, [("int",) + what], quantize, what, E4M3)
+
+        def PE_g(grp, pas, jp):
+            put("pe", ("trg", grp, pas, jp), [("raw", "g", grp, jp)], g_transpose, grp, pas, jp)
+
+        def C_g(grp, pas, jp, e="s"):
+            put(e, ("cg", grp, pas, jp), [("trg", grp, pas, jp)], copy_transposed, ("g", grp, pas), jp, e)
+
+        def V_qg(grp, pas, jp):
+            put("v", ("q", "g", grp, pas, jp), [("cg", grp, pas, jp)], quantize, ("g", grp, pas), E5M2, jp, 2)
+
+        def PE_dc(k, t):
+            grp, h = units[k]
+            put("pe", ("dc", k, t), [("q", "g", grp, p, t // 2) for p in range(N_P)] + [("q", "w2", h, p) for p in range(N_P)], dc, grp, h, t)
+
+        def V_m(k, t):
+            put("v", ("m", k, t), [("dc", k, t), ("raw", "z") + units[k]], mask, units[k][0], units[k][1], t)
+
+        def PE_tr(k):
+            for jp in range(2):
+                put("pe", ("trb", k, jp), [("m", k, 2 * jp + 1)], b_transpose, units[k][0], units[k][1], jp)
+
+        def C_b(k, e="s"):
+            for jp in range(2):
+                put(e, ("cb", k, jp), [("trb", k, jp)], copy_transposed, ("b",) + units[k], jp, e)
+
+        def V_qB(k):
+            put("v", ("q", "b") + units[k], [("cb", k, 1)], quantize, ("b",) + units[k], E5M2)
+
+        def V_intA(k):
+            put("v", ("ia", k), [("m", k, 3)], int_a, units[k][0], units[k][1])
+
+        def V_qA(k):
+            put("v", ("q", "a") + units[k], [("ia", k)], quantize, ("a",) + units[k], E5M2)
+
+        def needs_of(terms):
+            r = []
+            for lhs, rhs in terms:
+                if lhs[0] == "g":
+                    r.extend([("q",) + lhs + (jp,) for jp in range(2)])
+                else:
+                    r.append(("q",) + lhs)
+                r.append(("q",) + rhs)
+            return r
+
+        def PE_job(key, terms, t, where):
+            put("pe", ("pe",) + key, needs_of(terms), product, key, terms, t, where)
+
+        def E_job(key, t, e):
+            put(e, ("ev",) + key[:2] + (t,), [("pe",) + key], evac, key, t, e)
+
+        def A_job(key, t):
+            put("v", ("ad",) + key[:2] + (t,), [("pe",) + key, ("ev",) + key[:2] + (t,)], evac_add, key, t)
+
+        def ST(key, t, n, kind):
+            put("store", ("st",) + key + (t,), [(kind,) + key + (i,) for i in range(t, t + n)], store, key, t, n)
+
+        def job(name, where, e):
+            if name[0] == "o1":
+                h, c = name[1:]
+                terms = [(("a", grp, h), ("x", grp)) for grp in range(N_G)]
+                PE_job(name, terms, c, where)
+                E_job(name, c, e)
+                if c % 2 == 1:
+                    ST(name[:2], c - 1, 2, "ev")
+            else:
+                grp, t, stage = name[1:]
+                stages = MODES[grp, t]
+                PE_job(("o0", grp, t, stage), out0_terms(grp, stages[stage]), t, where)
+                if stage == 0:
+                    E_job(("o0", grp, t, 0), t, e)
+                else:
+                    A_job(("o0", grp, t, stage), t)
+                if stage == len(stages) - 1 and t % 2 == 1:
+                    ST(("o0", grp), t - 1, 2, "ev" if stage == 0 else "ad")
+
+
+        seq = [("w2", 0, 0), ("g", 0, 0), ("w2", 0, 1), ("g", 0, 1), ("z", 0, 0), ("w2", 1, 0), ("g", 1, 0), ("g", 1, 1), ("z", 1, 0), ("w2", 1, 1), ("x", 0), ("x", 1), ("z", 0, 1),
+               ("w2", 2, 0), ("w2", 2, 1), ("z", 1, 1), ("w2x", 0), ("w2x", 1), ("w1", 0), ("w1", 1), ("z", 0, 2), ("z", 1, 2), ("w2", 3, 0), ("w2", 3, 1), ("z", 0, 3), ("w1", 2), ("w1", 3), ("z", 1, 3)]
+        for i, what in enumerate(seq):
+            need = [] if i < 13 else [("m", (i - 13) // 3, 1)]
+            L(what, need)
+
+        for jp in range(2):
+            for pas in range(N_P):
+                PE_g(0, pas, jp)
+                C_g(0, pas, jp)
+        V_int(("w2", 0, 0))
+        V_qg(0, 0, 0)
+        V_qg(0, 1, 0)
+        V_q(("w2", 0, 0))
+        V_int(("w2", 0, 1))
+        V_qg(0, 0, 1)
+        V_q(("w2", 0, 1))
+        V_qg(0, 1, 1)
+        PE_dc(0, 0)
+        PE_dc(0, 1)
+
+        steps = {
+            0: dict(v=[], s=[("w2", 1, 0)], j=[]),
+            1: dict(v=[("i", ("w2", 1, 1)), ("q", ("w2", 1, 0)), ("q", ("w2", 1, 1))], s=[("x", 0), ("x", 1)], j=[]),
+            2: dict(v=[("q", ("x", 0)), ("q", ("x", 1)), ("i", ("w2", 2, 0)), ("q", ("w2", 2, 0))], s=[("w2", 2, 1), ("w2x", 0)], j=[]),
+            3: dict(v=[("q", ("w2", 2, 1)), ("i", ("w2x", 1)), ("q", ("w2x", 0)), ("q", ("w2x", 1))], s=[("w1", 0), ("w1", 1)], j=[("o1", 0, c) for c in range(4)]),
+            4: dict(v=[("q", ("w1", 0)), ("q", ("w1", 1))], s=[("w2", 3, 0), ("w2", 3, 1)], j=[("o0", 0, t, 0) for t in range(3)]),
+            5: dict(v=[("q", ("w2", 3, 0)), ("q", ("w2", 3, 1))], s=[("w1", 2)], j=[("o0", 0, 3, 0)] + [("o1", 1, c) for c in range(4)]),
+            6: dict(v=[("q", ("w1", 2))], s=[("w1", 3)], j=[("o0", 1, t, 0) for t in range(4)]),
+            7: dict(v=[("q", ("w1", 3))], s=[], j=[("o1", 2, c) for c in range(4)] + [("o0", 0, t, 1) for t in range(0)]),
+        }
+        for k in range(len(units)):
+            todo = list(steps[k]["j"])
+            vs = list(steps[k]["v"])
+            ss = list(steps[k]["s"])
+            if k > 0:
+                vs = vs[:1] + [("qa", k - 1)] + vs[1:2] + [("qb", k - 1)] + vs[2:]
+            nper = [len(vs) // 4 + (1 if i < len(vs) % 4 else 0) for i in range(4)]
+            early = len(todo) - 1 if len(todo) > 1 else 0
+            jper = [0] + [early // 3 + (1 if i >= 3 - early % 3 else 0) for i in range(3)]
+            for t in range(4):
+                V_m(k, t)
+                for i in range(nper[t]):
+                    it = vs.pop(0)
+                    if it[0] == "qb":
+                        V_qB(it[1])
+                    elif it[0] == "qa":
+                        V_qA(it[1])
+                    elif it[0] == "q":
+                        V_q(it[1])
+                    elif it[0] == "i":
+                        V_int(it[1])
+                    else:
+                        V_qg(it[1], 0, it[2])
+                        V_qg(it[1], 1, it[2])
+                if t < 2:
+                    PE_dc(k, t + 2)
+                if ss and t in (0, 2):
+                    S_int(ss.pop(0))
+                if k == 0 and t == 0:
+                    for jp in range(2):
+                        for pas in range(N_P):
+                            C_g(1, pas, jp)
+                if k == 0 and t == 1:
+                    for jp in range(2):
+                        for pas in range(N_P):
+                            PE_g(1, pas, jp)
+                for i in range(jper[t]):
+                    job(todo.pop(0), ps_out, "s")
+            if k + 1 < len(units):
+                PE_dc(k + 1, 0)
+            PE_tr(k)
+            C_b(k)
+            for it in todo:
+                job(it, ps_out, "s")
+            V_intA(k)
+            if k == 0:
+                for jp in range(2):
+                    for pas in range(N_P):
+                        V_qg(1, pas, jp)
+            if k + 1 < len(units):
+                PE_dc(k + 1, 1)
+        last = len(units) - 1
+        for t in range(4):
+            job(("o0", 0, t, 1), ps_dc if t % 2 else ps_out, "v")
+            if t == 0:
+                V_qA(last)
+            if t == 1:
+                V_qB(last)
+        for c in range(4):
+            job(("o1", 3, c), ps_dc if c % 2 else ps_out, "s")
+        for t in range(4):
+            job(("o0", 1, t, 1), ps_dc if t % 2 else ps_out, "v")
+
+
+        done = set()
+        order = ["load", "v", "s", "store", "pe"]
+        while any([len(q) > 0 for q in queues.values()]):
+            ready = [n for n in order if queues[n] and all([need in done for need in queues[n][0][1]])]
+            assert ready, [q[0][:2] for q in queues.values() if q]
+            name, needs, fn, args = queues[ready[0]].pop(0)
+            fn(*args)
+            done.add(name)

@@ -26,6 +26,44 @@ N_H = HID // W
 N_P = OUT // W
 
 
+ORDERS = {
+    "pe": (
+    "trg.0.0.0 trg.0.1.0 trg.0.1.1 trg.0.0.1 trg.1.0.1 trg.1.1.1 dc.2.1 dc.2.0 dc.2.3 dc.2.2 dc.0.1 dc.0.3 trg.1.1.0 trg.1.0.0 dc.0.2 trb.2.0 dc.0.0 "
+    "trb.2.1 dc.3.2 dc.1.3 dc.3.1 dc.3.3 trb.0.0 trb.0.1 dc.3.0 dc.1.2 dc.1.0 trb.3.0 dc.1.1 trb.3.1 pe.o1.1.3.term.0 pe.o1.1.2.term.0 pe.o1.1.3 "
+    "pe.o1.1.2 pe.o1.1.0.term.0 pe.o1.1.0 trb.1.1 pe.o1.0.0.term.0 trb.1.0 pe.o1.1.1.term.0 pe.o1.1.1 dc.4.1 dc.4.3 dc.4.2 dc.5.1 pe.o1.0.1.term.0 "
+    "dc.4.0 dc.5.2 trb.4.1 trb.4.0 pe.o1.0.3.term.0 pe.o1.0.0 pe.o1.0.1 pe.o1.0.2.term.0 pe.o1.0.3 dc.5.0 dc.5.3 pe.o1.0.2 dc.6.3 dc.6.2 dc.6.0 "
+    "trb.5.0 pe.o1.2.2.term.0 dc.7.3 dc.7.1 dc.6.1 trb.6.1 trb.5.1 dc.7.0 dc.7.2 pe.o1.2.2 pe.o1.2.0.term.0 pe.o1.2.0 pe.o1.2.3.term.0 pe.o1.2.3 "
+    "pe.o1.2.1.term.0 pe.o1.2.1 trb.7.1 pe.o0.1.1.0.term.0 pe.o0.0.3.0.term.0 pe.o0.0.3.0.term.1 pe.o0.0.1.0.term.0 pe.o0.0.1.0.term.1 "
+    "pe.o0.1.0.0.term.0 pe.o0.1.0.0.term.1 pe.o0.1.1.0.term.1 pe.o0.0.3.0.term.2 pe.o0.0.1.0.term.2 pe.o0.1.1.0.term.2 pe.o0.0.0.0.term.0 "
+    "pe.o0.1.0.0.term.2 pe.o0.0.0.0.term.1 pe.o0.0.0.0.term.2 trb.6.0 trb.7.0 pe.o0.1.0.0.term.3 pe.o0.0.2.0.term.0 pe.o0.1.1.0.term.3 "
+    "pe.o0.0.1.0.term.3 pe.o0.0.2.0.term.1 pe.o0.0.0.0.term.3 pe.o0.0.2.0.term.2 pe.o0.1.1.0.term.4 pe.o0.0.3.0.term.3 pe.o0.0.3.0.term.4 "
+    "pe.o0.1.0.0.term.4 pe.o0.0.0.0.term.4 pe.o0.0.2.0.term.3 pe.o0.0.2.0.term.4 pe.o0.0.0.0 pe.o0.0.2.0 pe.o0.0.3.0 pe.o0.1.0.0 pe.o0.1.1.0 "
+    "pe.o0.0.1.0.term.4 pe.o0.1.3.0.term.0 pe.o0.1.2.0.term.0 pe.o0.1.2.0.term.1 pe.o0.0.1.0 pe.o1.3.2.term.0 pe.o1.3.1.term.0 pe.o1.3.2 "
+    "pe.o1.3.3.term.0 pe.o1.3.3 pe.o1.3.1 pe.o1.3.0.term.0 pe.o0.1.2.0.term.2 pe.o1.3.0 pe.o0.1.3.0.term.1 pe.o0.1.2.0.term.3 pe.o0.1.3.0.term.2 "
+    "pe.o0.1.2.0.term.4 pe.o0.1.2.0 pe.o0.1.3.0.term.3 pe.o0.1.3.0.term.4 pe.o0.1.3.0 "
+    ),
+    "v": (
+    "int.w2.1.1 cg.0.1.0 q.g.0.1.0 q.g.0.0.0 cg.0.1.1 q.g.0.0.1 q.w2.1.1 int.w2.1.0 q.g.0.1.1 q.w2.1.0 q.w2.0.1 int.w2.0.0 q.g.1.0.1 q.w2.0.0 "
+    "q.g.1.1.1 m.2.2 m.2.1 m.2.0 m.2.3 ia.2 q.g.1.1.0 q.a.0.1 q.g.1.0.0 m.0.0 m.0.2 m.0.1 m.0.3 q.x.1 ia.0 m.3.2 m.3.1 m.3.0 q.x.0 q.a.0.0 m.3.3 ia.3 "
+    "q.w2.2.1 q.a.1.1 m.1.3 m.1.2 m.1.1 m.1.0 q.w2.2.0 ia.1 q.b.1.1 m.4.1 m.4.3 m.4.2 q.a.1.0 m.4.0 q.b.0.0 q.w2.3.0 m.5.1 q.w2.3.1 ia.4 m.5.0 m.5.2 "
+    "q.a.0.2 m.6.3 q.b.0.1 m.6.2 m.5.3 ia.5 m.6.1 q.a.1.2 m.6.0 m.7.3 m.7.2 q.w2x.0 m.7.1 q.w2x.1 ev.o1.2.2 q.w1.0 q.b.1.0 m.7.0 q.b.0.2 q.b.1.2 "
+    "q.w1.1 int.w1.2 q.w1.2 q.b.0.3 ia.7 q.w1.3 q.b.1.3 ia.6 q.a.0.3 q.a.1.3 ev.o1.3.2 "
+    ),
+    "s": (
+    "cg.0.0.0 cg.0.0.1 int.w2.0.1 cg.1.0.1 cg.1.1.1 cg.1.1.0 cg.1.0.0 int.x.1 cb.2.1 cb.2.0 int.x.0 cb.0.0 cb.0.1 int.w2.2.1 cb.3.0 int.w2.2.0 cb.3.1 "
+    "ev.o1.1.3 int.w2.3.0 ev.o1.1.1 ev.o1.1.2 cb.1.0 cb.1.1 int.w2.3.1 ev.o1.1.0 cb.4.1 ev.o1.0.0 ev.o1.0.3 int.w2x.1 ev.o1.0.1 cb.4.0 ev.o1.0.2 "
+    "cb.5.0 int.w2x.0 cb.5.1 int.w1.0 ev.o1.2.0 ev.o1.2.1 int.w1.1 cb.7.1 cb.6.1 ev.o1.2.3 cb.6.0 int.w1.3 cb.7.0 ev.o0.0.0 ev.o0.0.3 ev.o0.1.1 "
+    "ev.o0.1.0 ev.o0.0.2 ev.o0.0.1 ev.o1.3.3 ev.o1.3.1 ev.o1.3.0 ev.o0.1.2 ev.o0.1.3 "
+    ),
+    "load": (
+    "raw.g.0.0 raw.w2.1.1 raw.g.0.1 raw.w2.0.1 raw.w2.1.0 raw.g.1.1 raw.w2.0.0 raw.z.0.1 raw.g.1.0 raw.x.1 raw.z.0.0 raw.x.0 raw.z.1.1 raw.w2.2.1 "
+    "raw.w2.2.0 raw.z.1.0 raw.w2.3.0 raw.z.0.2 raw.w2.3.1 raw.z.1.2 raw.w2x.1 raw.z.0.3 raw.w2x.0 raw.z.1.3 raw.w1.0 st.o1.1.0 st.o1.1.2 raw.w1.1 "
+    "raw.w1.3 raw.w1.2 st.o1.0.0 st.o1.0.2 st.o1.2.0 st.o1.2.2 st.o0.0.0 st.o0.0.3 st.o0.1.1 st.o0.1.0 st.o0.0.2 st.o0.0.1 st.o1.3.2 st.o1.3.0 "
+    "st.o0.1.2 st.o0.1.3 "
+    ),
+}
+
+
 def tile_dpn_v_kernel(tc, x, W1, b1, W2, b2, z1, grad_out, out_0, out_1):
     nc = tc.nc
 
@@ -47,10 +85,8 @@ def tile_dpn_v_kernel(tc, x, W1, b1, W2, b2, z1, grad_out, out_0, out_1):
         a_pool = pool("a_pool", 5)
         b_pool = pool("b_pool", 8)
         out_pool = pool("out_pool", 2)
-        out0_pool = pool("out0_pool", 2)
-        ps_dc = ctx.enter_context(tc.psum_pool(name="ps_dc", bufs=3))
+        ps_mm = ctx.enter_context(tc.psum_pool(name="ps_mm", bufs=6))
         ps_tr = ctx.enter_context(tc.psum_pool(name="ps_tr", bufs=2))
-        ps_out = ctx.enter_context(tc.psum_pool(name="ps_out", bufs=3))
 
         ident = const.tile([P, P], F32, name="ident", align_bytes=64)
         make_identity(nc, ident[:])
@@ -76,7 +112,7 @@ def tile_dpn_v_kernel(tc, x, W1, b1, W2, b2, z1, grad_out, out_0, out_1):
             queues[queue].append((name, needs, fn, args))
 
         def load_g(grp, jp):
-            if jp == 0:
+            if ("g", grp) not in raws:
                 raws["g", grp] = graw_pool.tile([P, PACK, OUT], BF16, name="graw", align_bytes=64)
             t = raws["g", grp]
             nc.sync.dma_start(out=t[:, 2 * jp : 2 * jp + 2, :], in_=g_rows[grp, :, 2 * jp : 2 * jp + 2, :])
@@ -97,7 +133,7 @@ def tile_dpn_v_kernel(tc, x, W1, b1, W2, b2, z1, grad_out, out_0, out_1):
                 src = x_rows[what[1]]
             t = raw_pool.tile([P, PACK, W], BF16, name="raw", align_bytes=64)
             nc.sync.dma_start(out=t[:], in_=src)
-            raws[what] = t
+            raws[what] = t[:]
 
         def new_codes(key):
             src, tag = keep, "_".join([str(v) for v in key])
@@ -108,7 +144,7 @@ def tile_dpn_v_kernel(tc, x, W1, b1, W2, b2, z1, grad_out, out_0, out_1):
             codes[key] = (c, s)
 
         def quantize(key, fmt, part=0, parts=1):
-            if part == 0:
+            if key not in codes:
                 new_codes(key)
             c, s = codes[key]
             cols = slice(part * (W // parts), (part + 1) * (W // parts))
@@ -117,8 +153,10 @@ def tile_dpn_v_kernel(tc, x, W1, b1, W2, b2, z1, grad_out, out_0, out_1):
                 out=c[:, cols].bitcast(fmt), scales=s[:, cols], in_=groups[key][:].rearrange("p w k -> p (w k)")[:, wide]
             )
 
+        now = {}
+
         def copy(engine, out, in_):
-            if engine == "s":
+            if now["engine"] == "s":
                 nc.scalar.copy(out=out, in_=in_)
             else:
                 nc.vector.tensor_copy(out=out, in_=in_)
@@ -127,11 +165,11 @@ def tile_dpn_v_kernel(tc, x, W1, b1, W2, b2, z1, grad_out, out_0, out_1):
             raw = raws[what]
             grp = grp_pool.tile([P, W, PACK], BF16, name="grp", align_bytes=64)
             if what[0] == "w2":
-                dst = grp[:].rearrange("p (u q e) k -> p u q e k", u=2, e=2)
-                src = raw[:].rearrange("p k (q u e) -> p u q e k", u=2, e=2)
+                dst = grp[:].rearrange("p (u q e) k -> p q k u e", u=2, e=2)
+                src = raw.rearrange("p k (q u e) -> p q k u e", u=2, e=2)
             else:
-                dst = grp[:]
-                src = raw[:].rearrange("p k w -> p w k")
+                dst = grp[:].rearrange("p (q i) k -> p q k i", i=4)
+                src = raw.rearrange("p k (q i) -> p q k i", i=4)
             copy(engine, dst, src)
             groups[what] = grp
 
@@ -152,7 +190,7 @@ def tile_dpn_v_kernel(tc, x, W1, b1, W2, b2, z1, grad_out, out_0, out_1):
             transpose_bank(("b", grp, h, jp), w, [(2 * jp + jj) * (W // 2) for jj in range(2)], 1)
 
         def copy_transposed(key, jp, engine):
-            if jp == 0:
+            if key not in groups:
                 groups[key] = grpb_pool.tile([P, W, PACK], BF16, name="gb", align_bytes=64)
             dst = groups[key][:].rearrange("p r k -> p (r k)").bitcast(F32)[:, jp * W : (jp + 1) * W]
             copy(engine, dst.rearrange("p (r u) -> p r u", u=2), banks[key + (jp,)][:].rearrange("p u r -> p r u"))
@@ -172,13 +210,13 @@ def tile_dpn_v_kernel(tc, x, W1, b1, W2, b2, z1, grad_out, out_0, out_1):
             )
 
         def dc(grp, h, t):
-            bank = ps_dc.tile([P, W], F32, name="dcb")
+            bank = ps_mm.tile([P, W], F32, name="mm")
             for pas in range(N_P):
                 mx(bank, ("g", grp, pas), t, ("w2", h, pas), pas == 0, pas == N_P - 1)
             banks["dc", grp, h, t] = bank
 
         def mask(grp, h, t):
-            if t == 0:
+            if ("dz", grp, h) not in groups:
                 groups["dz", grp, h] = dz_pool.tile([P, PACK, W], BF16, name="dz", align_bytes=64)
             dz = groups["dz", grp, h]
             bank = banks["dc", grp, h, t]
@@ -196,23 +234,22 @@ def tile_dpn_v_kernel(tc, x, W1, b1, W2, b2, z1, grad_out, out_0, out_1):
 
         def int_a(grp, h):
             ga = grpa_pool.tile([P, W, PACK], BF16, name="ga", align_bytes=64)
-            nc.vector.tensor_copy(
-                out=ga[:].rearrange("p (u e q) t -> p u e q t", u=2, e=2),
-                in_=groups["dz", grp, h][:].rearrange("p t (u q e) -> p u e q t", u=2, e=2),
-            )
+            dst = ga[:].rearrange("p (u e q i) t -> p u q t i e", u=2, e=2, i=2)
+            src = groups["dz", grp, h][:].rearrange("p t (u q i e) -> p u q t i e", u=2, e=2, i=2)
+            for u in range(2):
+                nc.vector.tensor_copy(out=dst[:, u], in_=src[:, u])
             groups["a", grp, h] = ga
 
         outs = {}
 
-        def product(key, terms, t, last_pool):
-            bank = last_pool.tile([P, W], F32, name="dcb" if last_pool is ps_dc else "ob")
-            for i, (lhs, rhs) in enumerate(terms):
-                mx(bank, lhs, t, rhs, i == 0, i == len(terms) - 1)
-            banks[key] = bank
+        def product_term(key, terms, t, i):
+            if i == 0:
+                banks[key] = ps_mm.tile([P, W], F32, name="mm")
+            mx(banks[key], terms[i][0], t, terms[i][1], i == 0, i == len(terms) - 1)
 
         def out_tile(key):
             if key not in outs:
-                outs[key] = (out_pool if key[0] == "o1" else out0_pool).tile([P, PACK, D_IN], F32, name=key[0], align_bytes=64)
+                outs[key] = (out_pool.tile([P, PACK, D_IN], F32, name="o1", align_bytes=64) if key[0] == "o1" else graw_pool.tile([P, PACK, D_IN], F32, name="graw", align_bytes=64))
             return outs[key]
 
         def evac(key, t, engine):
@@ -236,7 +273,7 @@ def tile_dpn_v_kernel(tc, x, W1, b1, W2, b2, z1, grad_out, out_0, out_1):
             return r
 
 
-        MODES = {(grp, t): [["x", 0, 1], [2, 3]] for grp in range(2) for t in range(4)}
+        MODES = {(grp, t): [["x", 0, 1, 2, 3]] for grp in range(2) for t in range(4)}
         units = [(k % 2, k // 2) for k in range(2 * N_H)]
 
         def L(what, needs=()):
@@ -247,11 +284,14 @@ def tile_dpn_v_kernel(tc, x, W1, b1, W2, b2, z1, grad_out, out_0, out_1):
             else:
                 put("load", ("raw",) + what, needs, load_w, what)
 
+        def loaded_as(what):
+            return what
+
         def V_int(what):
-            put("v", ("int",) + what, [("raw",) + what], interleave, what, "v")
+            put("v", ("int",) + what, [("raw",) + loaded_as(what)], interleave, what, "v")
 
         def S_int(what):
-            put("s", ("int",) + what, [("raw",) + what], interleave, what, "s")
+            put("s", ("int",) + what, [("raw",) + loaded_as(what)], interleave, what, "s")
 
         def V_q(what):
             put("v", ("q",) + what, [("int",) + what], quantize, what, E4M3)
@@ -274,17 +314,17 @@ def tile_dpn_v_kernel(tc, x, W1, b1, W2, b2, z1, grad_out, out_0, out_1):
 
         def PE_tr(k):
             for jp in range(2):
-                put("pe", ("trb", k, jp), [("m", k, 2 * jp + 1)], b_transpose, units[k][0], units[k][1], jp)
+                put("pe", ("trb", k, jp), [("m", k, 2 * jp), ("m", k, 2 * jp + 1)], b_transpose, units[k][0], units[k][1], jp)
 
         def C_b(k, e="s"):
             for jp in range(2):
                 put(e, ("cb", k, jp), [("trb", k, jp)], copy_transposed, ("b",) + units[k], jp, e)
 
         def V_qB(k):
-            put("v", ("q", "b") + units[k], [("cb", k, 1)], quantize, ("b",) + units[k], E5M2)
+            put("v", ("q", "b") + units[k], [("cb", k, 0), ("cb", k, 1)], quantize, ("b",) + units[k], E5M2)
 
         def V_intA(k):
-            put("v", ("ia", k), [("m", k, 3)], int_a, units[k][0], units[k][1])
+            put("v", ("ia", k), [("m", k, t) for t in range(4)], int_a, units[k][0], units[k][1])
 
         def V_qA(k):
             put("v", ("q", "a") + units[k], [("ia", k)], quantize, ("a",) + units[k], E5M2)
@@ -300,7 +340,9 @@ def tile_dpn_v_kernel(tc, x, W1, b1, W2, b2, z1, grad_out, out_0, out_1):
             return r
 
         def PE_job(key, terms, t, where):
-            put("pe", ("pe",) + key, needs_of(terms), product, key, terms, t, where)
+            for i in range(len(terms)):
+                n = ("pe",) + key + (() if i == len(terms) - 1 else ("term", i))
+                put("pe", n, needs_of(terms[i : i + 1]) + ([("pe",) + key + ("term", i - 1)] if i else []), product_term, key, terms, t, i)
 
         def E_job(key, t, e):
             put(e, ("ev",) + key[:2] + (t,), [("pe",) + key], evac, key, t, e)
@@ -322,13 +364,16 @@ def tile_dpn_v_kernel(tc, x, W1, b1, W2, b2, z1, grad_out, out_0, out_1):
             else:
                 grp, t, stage = name[1:]
                 stages = MODES[grp, t]
-                PE_job(("o0", grp, t, stage), out0_terms(grp, stages[stage]), t, where)
+                key = ("o0", grp, t, stage)
+                PE_job(key, out0_terms(grp, stages[stage]), t, where)
                 if stage == 0:
                     E_job(("o0", grp, t, 0), t, e)
                 else:
                     A_job(("o0", grp, t, stage), t)
-                if stage == len(stages) - 1 and t % 2 == 1:
-                    ST(("o0", grp), t - 1, 2, "ev" if stage == 0 else "ad")
+                if grp == 1 and stage == len(stages) - 1:
+                    ST(("o0", grp), t, 1, "ev" if stage == 0 else "ad")
+                elif stage == len(stages) - 1:
+                    ST(("o0", grp), t, 1, "ev" if stage == 0 else "ad")
 
 
         seq = [("w2", 0, 0), ("g", 0, 0), ("w2", 0, 1), ("g", 0, 1), ("z", 0, 0), ("w2", 1, 0), ("g", 1, 0), ("g", 1, 1), ("z", 1, 0), ("w2", 1, 1), ("x", 0), ("x", 1), ("z", 0, 1),
@@ -360,10 +405,10 @@ def tile_dpn_v_kernel(tc, x, W1, b1, W2, b2, z1, grad_out, out_0, out_1):
             4: dict(v=[("q", ("w1", 0)), ("q", ("w1", 1))], s=[("w2", 3, 0), ("w2", 3, 1)], j=[("o0", 0, t, 0) for t in range(3)]),
             5: dict(v=[("q", ("w2", 3, 0)), ("q", ("w2", 3, 1))], s=[("w1", 2)], j=[("o0", 0, 3, 0)] + [("o1", 1, c) for c in range(4)]),
             6: dict(v=[("q", ("w1", 2))], s=[("w1", 3)], j=[("o0", 1, t, 0) for t in range(4)]),
-            7: dict(v=[("q", ("w1", 3))], s=[], j=[("o1", 2, c) for c in range(4)] + [("o0", 0, t, 1) for t in range(0)]),
+            7: dict(v=[("q", ("w1", 3))], s=[], j=[("o1", 2, c) for c in range(4)] + [("o0", 0, t, len(MODES[0, t]) - 1) for t in range(0)]),
         }
         for k in range(len(units)):
-            todo = list(steps[k]["j"])
+            todo = [j for j in steps[k]["j"] if not (j[0] == "o0" and len(MODES[j[1], j[2]]) == 1)]
             vs = list(steps[k]["v"])
             ss = list(steps[k]["s"])
             if k > 0:
@@ -399,13 +444,13 @@ def tile_dpn_v_kernel(tc, x, W1, b1, W2, b2, z1, grad_out, out_0, out_1):
                         for pas in range(N_P):
                             PE_g(1, pas, jp)
                 for i in range(jper[t]):
-                    job(todo.pop(0), ps_out, "s")
+                    job(todo.pop(0), None, "s")
             if k + 1 < len(units):
                 PE_dc(k + 1, 0)
             PE_tr(k)
             C_b(k)
             for it in todo:
-                job(it, ps_out, "s")
+                job(it, None, "s")
             V_intA(k)
             if k == 0:
                 for jp in range(2):
@@ -415,22 +460,24 @@ def tile_dpn_v_kernel(tc, x, W1, b1, W2, b2, z1, grad_out, out_0, out_1):
                 PE_dc(k + 1, 1)
         last = len(units) - 1
         for t in range(4):
-            job(("o0", 0, t, 1), ps_dc if t % 2 else ps_out, "v")
+            job(("o0", 0, t, len(MODES[0, t]) - 1), None, "v")
             if t == 0:
                 V_qA(last)
             if t == 1:
                 V_qB(last)
         for c in range(4):
-            job(("o1", 3, c), ps_dc if c % 2 else ps_out, "s")
+            job(("o1", 3, c), None, "s")
         for t in range(4):
-            job(("o0", 1, t, 1), ps_dc if t % 2 else ps_out, "v")
+            job(("o0", 1, t, len(MODES[1, t]) - 1), None, "v")
 
 
+        by_name = {".".join([str(v) for v in op[0]]): (op[0], [] if op[0][0] == "raw" else op[1], op[2], op[3]) for q in queues.values() for op in q}
+        queues = {e: [by_name[n] for n in ORDERS[e].split()] for e in ORDERS}
         done = set()
-        order = ["load", "v", "s", "store", "pe"]
         while any([len(q) > 0 for q in queues.values()]):
-            ready = [n for n in order if queues[n] and all([need in done for need in queues[n][0][1]])]
-            assert ready, [q[0][:2] for q in queues.values() if q]
+            ready = [n for n in ("load", "v", "s", "pe") if queues[n] and all([need in done for need in queues[n][0][1]])]
+            assert ready, [(q[0][0], [n for n in q[0][1] if n not in done]) for q in queues.values() if q]
             name, needs, fn, args = queues[ready[0]].pop(0)
+            now["engine"] = ready[0]
             fn(*args)
             done.add(name)

@@ -14,53 +14,50 @@ U32 = mybir.dt.uint32
 U8 = mybir.dt.uint8
 E4M3 = mybir.dt.float8_e4m3fn_x4
 E5M2 = mybir.dt.float8_e5m2_x4
-IS_GT = mybir.AluOpType.is_gt
-MULT = mybir.AluOpType.mult
-ADD = mybir.AluOpType.add
 
 P = 128
 PACK = 4
-W = 512
-N_G = B // W
-N_H = HID // W
-N_P = OUT // W
+SPAN = P * PACK
+GROUPS = B // SPAN
+CHUNKS = HID // SPAN
+PASSES = OUT // SPAN
+ALIGN = 64
 
-
-ORDERS = {
-    "pe": (
-    "trg.0.0.0 trg.0.1.0 trg.0.1.1 trg.0.0.1 trg.1.0.1 trg.1.1.1 dc.2.1 dc.2.0 dc.2.3 dc.2.2 dc.0.1 dc.0.3 trg.1.1.0 trg.1.0.0 dc.0.2 trb.2.0 dc.0.0 "
-    "trb.2.1 dc.3.2 dc.1.3 dc.3.1 dc.3.3 trb.0.0 trb.0.1 dc.3.0 dc.1.2 dc.1.0 trb.3.0 dc.1.1 trb.3.1 pe.o1.1.3.term.0 pe.o1.1.2.term.0 pe.o1.1.3 "
-    "pe.o1.1.2 pe.o1.1.0.term.0 pe.o1.1.0 trb.1.1 pe.o1.0.0.term.0 trb.1.0 pe.o1.1.1.term.0 pe.o1.1.1 dc.4.1 dc.4.3 dc.4.2 dc.5.1 pe.o1.0.1.term.0 "
-    "dc.4.0 dc.5.2 trb.4.1 trb.4.0 pe.o1.0.3.term.0 pe.o1.0.0 pe.o1.0.1 pe.o1.0.2.term.0 pe.o1.0.3 dc.5.0 dc.5.3 pe.o1.0.2 dc.6.3 dc.6.2 dc.6.0 "
-    "trb.5.0 pe.o1.2.2.term.0 dc.7.3 dc.7.1 dc.6.1 trb.6.1 trb.5.1 dc.7.0 dc.7.2 pe.o1.2.2 pe.o1.2.0.term.0 pe.o1.2.0 pe.o1.2.3.term.0 pe.o1.2.3 "
-    "pe.o1.2.1.term.0 pe.o1.2.1 trb.7.1 pe.o0.1.1.0.term.0 pe.o0.0.3.0.term.0 pe.o0.0.3.0.term.1 pe.o0.0.1.0.term.0 pe.o0.0.1.0.term.1 "
-    "pe.o0.1.0.0.term.0 pe.o0.1.0.0.term.1 pe.o0.1.1.0.term.1 pe.o0.0.3.0.term.2 pe.o0.0.1.0.term.2 pe.o0.1.1.0.term.2 pe.o0.0.0.0.term.0 "
-    "pe.o0.1.0.0.term.2 pe.o0.0.0.0.term.1 pe.o0.0.0.0.term.2 trb.6.0 trb.7.0 pe.o0.1.0.0.term.3 pe.o0.0.2.0.term.0 pe.o0.1.1.0.term.3 "
-    "pe.o0.0.1.0.term.3 pe.o0.0.2.0.term.1 pe.o0.0.0.0.term.3 pe.o0.0.2.0.term.2 pe.o0.1.1.0.term.4 pe.o0.0.3.0.term.3 pe.o0.0.3.0.term.4 "
-    "pe.o0.1.0.0.term.4 pe.o0.0.0.0.term.4 pe.o0.0.2.0.term.3 pe.o0.0.2.0.term.4 pe.o0.0.0.0 pe.o0.0.2.0 pe.o0.0.3.0 pe.o0.1.0.0 pe.o0.1.1.0 "
-    "pe.o0.0.1.0.term.4 pe.o0.1.3.0.term.0 pe.o0.1.2.0.term.0 pe.o0.1.2.0.term.1 pe.o0.0.1.0 pe.o1.3.2.term.0 pe.o1.3.1.term.0 pe.o1.3.2 "
-    "pe.o1.3.3.term.0 pe.o1.3.3 pe.o1.3.1 pe.o1.3.0.term.0 pe.o0.1.2.0.term.2 pe.o1.3.0 pe.o0.1.3.0.term.1 pe.o0.1.2.0.term.3 pe.o0.1.3.0.term.2 "
-    "pe.o0.1.2.0.term.4 pe.o0.1.2.0 pe.o0.1.3.0.term.3 pe.o0.1.3.0.term.4 pe.o0.1.3.0 "
-    ),
-    "v": (
-    "int.w2.1.1 cg.0.1.0 q.g.0.1.0 q.g.0.0.0 cg.0.1.1 q.g.0.0.1 q.w2.1.1 int.w2.1.0 q.g.0.1.1 q.w2.1.0 q.w2.0.1 int.w2.0.0 q.g.1.0.1 q.w2.0.0 "
-    "q.g.1.1.1 m.2.2 m.2.1 m.2.0 m.2.3 ia.2 q.g.1.1.0 q.a.0.1 q.g.1.0.0 m.0.0 m.0.2 m.0.1 m.0.3 q.x.1 ia.0 m.3.2 m.3.1 m.3.0 q.x.0 q.a.0.0 m.3.3 ia.3 "
-    "q.w2.2.1 q.a.1.1 m.1.3 m.1.2 m.1.1 m.1.0 q.w2.2.0 ia.1 q.b.1.1 m.4.1 m.4.3 m.4.2 q.a.1.0 m.4.0 q.b.0.0 q.w2.3.0 m.5.1 q.w2.3.1 ia.4 m.5.0 m.5.2 "
-    "q.a.0.2 m.6.3 q.b.0.1 m.6.2 m.5.3 ia.5 m.6.1 q.a.1.2 m.6.0 m.7.3 m.7.2 q.w2x.0 m.7.1 q.w2x.1 ev.o1.2.2 q.w1.0 q.b.1.0 m.7.0 q.b.0.2 q.b.1.2 "
-    "q.w1.1 int.w1.2 q.w1.2 q.b.0.3 ia.7 q.w1.3 q.b.1.3 ia.6 q.a.0.3 q.a.1.3 ev.o1.3.2 "
-    ),
-    "s": (
-    "cg.0.0.0 cg.0.0.1 int.w2.0.1 cg.1.0.1 cg.1.1.1 cg.1.1.0 cg.1.0.0 int.x.1 cb.2.1 cb.2.0 int.x.0 cb.0.0 cb.0.1 int.w2.2.1 cb.3.0 int.w2.2.0 cb.3.1 "
-    "ev.o1.1.3 int.w2.3.0 ev.o1.1.1 ev.o1.1.2 cb.1.0 cb.1.1 int.w2.3.1 ev.o1.1.0 cb.4.1 ev.o1.0.0 ev.o1.0.3 int.w2x.1 ev.o1.0.1 cb.4.0 ev.o1.0.2 "
-    "cb.5.0 int.w2x.0 cb.5.1 int.w1.0 ev.o1.2.0 ev.o1.2.1 int.w1.1 cb.7.1 cb.6.1 ev.o1.2.3 cb.6.0 int.w1.3 cb.7.0 ev.o0.0.0 ev.o0.0.3 ev.o0.1.1 "
-    "ev.o0.1.0 ev.o0.0.2 ev.o0.0.1 ev.o1.3.3 ev.o1.3.1 ev.o1.3.0 ev.o0.1.2 ev.o0.1.3 "
-    ),
-    "load": (
-    "raw.g.0.0 raw.w2.1.1 raw.g.0.1 raw.w2.0.1 raw.w2.1.0 raw.g.1.1 raw.w2.0.0 raw.z.0.1 raw.g.1.0 raw.x.1 raw.z.0.0 raw.x.0 raw.z.1.1 raw.w2.2.1 "
-    "raw.w2.2.0 raw.z.1.0 raw.w2.3.0 raw.z.0.2 raw.w2.3.1 raw.z.1.2 raw.w2x.1 raw.z.0.3 raw.w2x.0 raw.z.1.3 raw.w1.0 st.o1.1.0 st.o1.1.2 raw.w1.1 "
-    "raw.w1.3 raw.w1.2 st.o1.0.0 st.o1.0.2 st.o1.2.0 st.o1.2.2 st.o0.0.0 st.o0.0.3 st.o0.1.1 st.o0.1.0 st.o0.0.2 st.o0.0.1 st.o1.3.2 st.o1.3.0 "
-    "st.o0.1.2 st.o0.1.3 "
-    ),
+QUEUES = {
+    "sync": [
+        "load.g.0.0 load.g.0.1 load.w2.0.0 load.w2.1.0 load.w2.0.1 load.w2.1.1 load.z.0.0.0 load.x.1 load.z.0.0.1",
+        "load.x.0 load.g.1.0 load.g.1.1 load.z.0.1.0 load.z.0.1.1 load.w2.2.0 load.z.1.0.1 load.z.1.0.0",
+        "load.w2.3.1 load.z.1.1.1 load.w2.2.1 load.z.1.1.0 load.z.0.2.1 load.z.0.2.0 load.w2.3.0 load.z.1.2.0",
+        "load.z.1.2.1 load.z.0.3.1 load.z.0.3.0 load.w2.x.0 load.z.1.3.0 load.w2.x.1 load.w1.0 load.z.1.3.1",
+        "store.dw.1.0 store.dw.1.1 load.w1.1 load.w1.2 load.w1.3 store.dw.0.1 store.dw.0.0 store.dw.2.0",
+        "store.dw.2.1 store.dx.0.0 store.dx.0.1 store.dx.1.0 store.dx.1.3 store.dx.1.1 store.dx.1.2 store.dw.3.0",
+        "store.dw.3.1 store.dx.0.2 store.dx.0.3",
+    ],
+    "vector": [
+        "q.g.0.0 copy.g.0.1 q.g.0.1 pack.w2.1.0 q.w2.0.0 pack.w2.0.1 q.w2.0.1 q.w2.1.0 mask.0.0.0 q.w2.1.1",
+        "mask.0.0.1 pack.token.0.0 q.x.1 q.token.0.0 q.x.0 q.g.1.0 mask.0.1.0 mask.0.1.1 q.g.1.1 pack.token.0.1",
+        "mask.1.0.1 mask.1.0.0 q.token.0.1 pack.token.1.0 q.w2.2.0 q.token.1.0 mask.1.1.1 mask.1.1.0 q.w2.3.1",
+        "q.w2.2.1 pack.token.1.1 mask.0.2.1 q.token.1.1 mask.0.2.0 mask.1.2.0 pack.token.0.2 mask.1.2.1 q.w2.3.0",
+        "pack.token.1.2 mask.0.3.0 mask.0.3.1 q.hidden.1.0 q.token.1.2 q.token.0.2 mask.1.3.0 mask.1.3.1 q.w2.x.0",
+        "q.w2.x.1 q.hidden.1.1 q.hidden.0.1 q.w1.0 q.hidden.0.3 pack.w1.1 q.hidden.0.0 q.w1.1 q.hidden.1.2",
+        "q.hidden.0.2 q.w1.2 pack.token.0.3 q.w1.3 q.hidden.1.3 pack.token.1.3 q.token.0.3 q.token.1.3 out.dx.1.2",
+        "out.dw.3.2 out.dw.3.3 out.dx.0.3",
+    ],
+    "scalar": [
+        "copy.g.0.0 pack.w2.0.0 pack.w2.1.1 pack.x.1 pack.x.0 copy.g.1.0 copy.g.1.1 copy.dz.0.0 copy.dz.0.1",
+        "pack.w2.2.0 pack.w2.3.1 copy.dz.1.0 pack.w2.2.1 out.dw.0.0 out.dw.0.3 copy.dz.1.1 out.dw.0.2 out.dw.0.1",
+        "pack.w2.3.0 out.dw.1.1 out.dw.1.0 copy.dz.0.2 out.dw.1.2 out.dw.1.3 copy.dz.1.2 pack.w2.x.0 pack.w2.x.1",
+        "copy.dz.0.3 pack.w1.0 out.dw.2.1 out.dw.2.0 out.dw.2.2 out.dw.2.3 pack.w1.2 pack.w1.3 copy.dz.1.3",
+        "out.dx.0.0 out.dx.0.1 out.dx.1.0 out.dx.1.3 out.dx.1.1 out.dw.3.0 out.dw.3.1 out.dx.0.2",
+    ],
+    "tensor": [
+        "turn.g.0.0 turn.g.0.1 dc.0.0.0 dc.0.0.1 dc.0.1.0 dc.0.1.1 turn.g.1.0 turn.g.1.1 turn.dz.0.0 turn.dz.0.1",
+        "dc.1.0.1 dc.1.0.0 dc.1.1.1 turn.dz.1.0 dc.1.1.0 dw.0.0 dw.0.1 turn.dz.1.1 dc.0.2.1 dc.1.2.0 dc.0.2.0",
+        "dw.1.0 turn.dz.0.2 dc.1.2.1 dw.1.1 turn.dz.1.2 dc.0.3.0 dc.0.3.1 dc.1.3.0 turn.dz.0.3 dc.1.3.1 dw.2.1",
+        "dw.2.0 turn.dz.1.3 dx.0.0.x dx.1.1.x dx.1.0.x dx.1.1.0 dx.1.0.0 dx.0.0.0 dx.0.0.1 dx.1.0.1 dx.1.1.1",
+        "dx.1.0.2 dx.1.1.2 dx.0.0.2 dx.0.0.3 dx.1.0.3 dx.1.1.3 dx.0.1.x dw.3.0 dw.3.1 dx.0.1.0 dx.0.1.1 dx.0.1.2",
+        "dx.0.1.3",
+    ],
 }
 
 
@@ -69,415 +66,284 @@ def tile_dpn_v_kernel(tc, x, W1, b1, W2, b2, z1, grad_out, out_0, out_1):
 
     with ExitStack() as ctx:
 
-        def pool(name, bufs):
+        def sbuf(name, bufs):
             return ctx.enter_context(tc.tile_pool(name=name, bufs=bufs))
 
-        const = pool("const", 1)
-        graw_pool = pool("graw_pool", 2)
-        raw_pool = pool("raw_pool", 6)
-        z_pool = pool("z_pool", 4)
-        dz_pool = pool("dz_pool", 3)
-        grp_pool = pool("grp_pool", 5)
-        grpa_pool = pool("grpa_pool", 2)
-        grpb_pool = pool("grpb_pool", 3)
-        keep = pool("keep", 1)
-        w2_pool = pool("w2_pool", 6)
-        a_pool = pool("a_pool", 5)
-        b_pool = pool("b_pool", 8)
-        out_pool = pool("out_pool", 2)
-        ps_mm = ctx.enter_context(tc.psum_pool(name="ps_mm", bufs=6))
-        ps_tr = ctx.enter_context(tc.psum_pool(name="ps_tr", bufs=2))
+        keep = sbuf("keep", 1)
+        big_pool = sbuf("big", 2)
+        raw_pool = sbuf("raw", 6)
+        z_pool = sbuf("z", 9)
+        dz_pool = sbuf("dz", 3)
+        packed_pool = sbuf("packed", 5)
+        by_token_pool = sbuf("by_token", 2)
+        turned_pool = sbuf("turned", 6)
+        w2_pool = sbuf("w2_codes", 6)
+        token_codes_pool = sbuf("token_codes", 5)
+        hidden_codes_pool = sbuf("hidden_codes", 8)
+        dw_pool = sbuf("dw", 2)
+        sums = ctx.enter_context(tc.psum_pool(name="sums", bufs=6))
+        turns = ctx.enter_context(tc.psum_pool(name="turns", bufs=2))
 
-        ident = const.tile([P, P], F32, name="ident", align_bytes=64)
-        make_identity(nc, ident[:])
+        identity = keep.tile([P, P], F32, name="identity", align_bytes=ALIGN)
+        make_identity(nc, identity[:])
 
         ctx.enter_context(tc.manual_schedule())
 
-        g_rows = grad_out.rearrange("(g p j) w -> g p j w", g=N_G, j=PACK)
-        z_rows = z1.rearrange("(g p j) h -> g p j h", g=N_G, j=PACK)
-        x_rows = x.rearrange("(g p j) d -> g p j d", g=N_G, j=PACK)
-        w2_rows = W2.rearrange("(g p j) c -> g p j c", g=N_P, j=PACK)
-        w1_rows = W1.rearrange("(g p j) d -> g p j d", g=N_H, j=PACK)
-        out0_rows = out_0.rearrange("(g p j) d -> g p j d", g=N_G, j=PACK)
-        out1_rows = out_1.rearrange("(h q c) d -> h q c d", h=N_H, c=PACK)
+        g_rows = grad_out.rearrange("(g p j) o -> g p j o", g=GROUPS, j=PACK)
+        z_rows = z1.rearrange("(g p j) h -> g p j h", g=GROUPS, j=PACK)
+        x_rows = x.rearrange("(g p j) d -> g p j d", g=GROUPS, j=PACK)
+        w2_rows = W2.rearrange("(i p j) c -> i p j c", i=PASSES, j=PACK)
+        w1_rows = W1.rearrange("(h p j) d -> h p j d", h=CHUNKS, j=PACK)
+        dx_rows = out_0.rearrange("(g p j) d -> g p j d", g=GROUPS, j=PACK)
+        dw_rows = out_1.rearrange("(h q c) d -> h q c d", h=CHUNKS, c=PACK)
 
-        raws = {}
-        groups = {}
+        loaded = {}
+        packed = {}
         codes = {}
+        masked = {}
         banks = {}
+        leaving = {}
 
-        queues = {"load": [], "pe": [], "v": [], "s": [], "store": []}
 
-        def put(queue, name, needs, fn, *args):
-            queues[queue].append((name, needs, fn, args))
+        def load_g(group, pair):
+            if group not in loaded:
+                loaded[group] = big_pool.tile([P, PACK, OUT], BF16, name="big", align_bytes=ALIGN)
+            rows = slice(2 * pair, 2 * pair + 2)
+            nc.sync.dma_start(out=loaded[group][:, rows, :], in_=g_rows[group, :, rows, :])
 
-        def load_g(grp, jp):
-            if ("g", grp) not in raws:
-                raws["g", grp] = graw_pool.tile([P, PACK, OUT], BF16, name="graw", align_bytes=64)
-            t = raws["g", grp]
-            nc.sync.dma_start(out=t[:, 2 * jp : 2 * jp + 2, :], in_=g_rows[grp, :, 2 * jp : 2 * jp + 2, :])
+        def load_z(group, chunk, pair):
+            tile = z_pool.tile([P, 2, SPAN], F32, name="z", align_bytes=ALIGN)
+            rows = slice(2 * pair, 2 * pair + 2)
+            nc.sync.dma_start(out=tile[:], in_=z_rows[group, :, rows, chunk * SPAN : (chunk + 1) * SPAN])
+            loaded["z", group, chunk, pair] = tile
 
-        def load_z(grp, h):
-            t = z_pool.tile([P, PACK, W], F32, name="zt", align_bytes=64)
-            nc.sync.dma_start(out=t[:], in_=z_rows[grp, :, :, h * W : (h + 1) * W])
-            raws["z", grp, h] = t
-
-        def load_w(what):
-            if what[0] == "w2":
-                src = w2_rows[what[2], :, :, D_IN + what[1] * W : D_IN + (what[1] + 1) * W]
-            elif what[0] == "w2x":
-                src = w2_rows[what[1], :, :, 0:D_IN]
-            elif what[0] == "w1":
-                src = w1_rows[what[1]]
+        def load_operand(key):
+            tile = raw_pool.tile([P, PACK, SPAN], BF16, name="raw", align_bytes=ALIGN)
+            if key[0] == "w2":
+                first = 0 if key[1] == "x" else D_IN + key[1] * SPAN
+                source = w2_rows[key[2], :, :, first : first + SPAN]
+            elif key[0] == "w1":
+                source = w1_rows[key[1]]
             else:
-                src = x_rows[what[1]]
-            t = raw_pool.tile([P, PACK, W], BF16, name="raw", align_bytes=64)
-            nc.sync.dma_start(out=t[:], in_=src)
-            raws[what] = t[:]
+                source = x_rows[key[1]]
+            nc.sync.dma_start(out=tile[:], in_=source)
+            loaded[key] = tile
 
-        def new_codes(key):
-            src, tag = keep, "_".join([str(v) for v in key])
-            if key[0] in ("w2", "a", "b"):
-                src, tag = {"w2": (w2_pool, "w2"), "a": (a_pool, "a"), "b": (b_pool, "b")}[key[0]]
-            c = src.tile([P, W], U32, name="c_" + tag, align_bytes=64)
-            s = src.tile([P, W], U8, name="s_" + tag, align_bytes=64)
-            codes[key] = (c, s)
-
-        def quantize(key, fmt, part=0, parts=1):
-            if key not in codes:
-                new_codes(key)
-            c, s = codes[key]
-            cols = slice(part * (W // parts), (part + 1) * (W // parts))
-            wide = slice(part * (PACK * W // parts), (part + 1) * (PACK * W // parts))
-            nc.vector.quantize_mx(
-                out=c[:, cols].bitcast(fmt), scales=s[:, cols], in_=groups[key][:].rearrange("p w k -> p (w k)")[:, wide]
-            )
-
-        now = {}
 
         def copy(engine, out, in_):
-            if now["engine"] == "s":
+            if engine == "scalar":
                 nc.scalar.copy(out=out, in_=in_)
             else:
                 nc.vector.tensor_copy(out=out, in_=in_)
 
-        def interleave(what, engine):
-            raw = raws[what]
-            grp = grp_pool.tile([P, W, PACK], BF16, name="grp", align_bytes=64)
-            if what[0] == "w2":
-                dst = grp[:].rearrange("p (u q e) k -> p q k u e", u=2, e=2)
-                src = raw.rearrange("p k (q u e) -> p q k u e", u=2, e=2)
+        def pack_operand(engine, key):
+            tile = packed_pool.tile([P, SPAN, PACK], BF16, name="packed", align_bytes=ALIGN)
+            source = loaded[key][:]
+            if key[0] == "w2" and key[1] != "x":
+                copy(
+                    engine,
+                    tile[:].rearrange("p (u q e) j -> p q j u e", u=2, e=2),
+                    source.rearrange("p j (q u e) -> p q j u e", u=2, e=2),
+                )
             else:
-                dst = grp[:].rearrange("p (q i) k -> p q k i", i=4)
-                src = raw.rearrange("p k (q i) -> p q k i", i=4)
-            copy(engine, dst, src)
-            groups[what] = grp
+                copy(
+                    engine,
+                    tile[:].rearrange("p (q i) j -> p q j i", i=4),
+                    source.rearrange("p j (q i) -> p q j i", i=4),
+                )
+            packed[key] = tile
 
-        def transpose_bank(key, w, starts, step):
-            bank = ps_tr.tile([P, 2, 256], F32, name="trb")
+        def pack_by_token(group, chunk):
+            tile = by_token_pool.tile([P, SPAN, PACK], BF16, name="by_token", align_bytes=ALIGN)
+            out = tile[:].rearrange("p (u e q i) j -> p u q j i e", u=2, e=2, i=2)
+            source = masked[group, chunk][:].rearrange("p j (u q i e) -> p u q j i e", u=2, i=2, e=2)
             for u in range(2):
-                for jj in range(2):
-                    o = starts[jj] + u * (1 if step == 2 else P)
-                    nc.tensor.transpose(bank[:, u, jj * P : (jj + 1) * P], w[:, o : o + step * (P - 1) + 1 : step], ident[:])
-            banks[key] = bank
+                nc.vector.tensor_copy(out=out[:, u], in_=source[:, u])
+            packed["token", group, chunk] = tile
 
-        def g_transpose(grp, pas, jp):
-            w = raws["g", grp][:].rearrange("p j w -> p (j w)").bitcast(F32)
-            transpose_bank(("g", grp, pas, jp), w, [(2 * jp + jj) * (OUT // 2) + pas * (W // 2) for jj in range(2)], 2)
+        def copy_turned(engine, key, pair):
+            if key not in packed:
+                packed[key] = turned_pool.tile([P, SPAN, PACK], BF16, name="turned", align_bytes=ALIGN)
+            words = packed[key][:].rearrange("p t k -> p (t k)").bitcast(F32)[:, pair * SPAN : (pair + 1) * SPAN]
+            copy(engine, words.rearrange("p (t u) -> p t u", u=2), banks[key + (pair,)][:].rearrange("p u t -> p t u"))
 
-        def b_transpose(grp, h, jp):
-            w = groups["dz", grp, h][:].rearrange("p t w -> p (t w)").bitcast(F32)
-            transpose_bank(("b", grp, h, jp), w, [(2 * jp + jj) * (W // 2) for jj in range(2)], 1)
+        def copy_g(engine, group, pair):
+            for i in range(PASSES):
+                copy_turned(engine, ("g", group, i), pair)
 
-        def copy_transposed(key, jp, engine):
-            if key not in groups:
-                groups[key] = grpb_pool.tile([P, W, PACK], BF16, name="gb", align_bytes=64)
-            dst = groups[key][:].rearrange("p r k -> p (r k)").bitcast(F32)[:, jp * W : (jp + 1) * W]
-            copy(engine, dst.rearrange("p (r u) -> p r u", u=2), banks[key + (jp,)][:].rearrange("p u r -> p r u"))
+        def copy_dz(engine, group, chunk):
+            for pair in range(2):
+                copy_turned(engine, ("hidden", group, chunk), pair)
 
-        def mx(bank, lhs, t, rhs, start, stop):
-            lc, ls = codes[lhs]
-            rc, rs = codes[rhs]
-            cols = slice(t * P, (t + 1) * P)
-            nc.tensor.matmul_mx(
-                out=bank[:],
-                lhsT=lc[:, cols].bitcast(E5M2),
-                lhsT_scale=ls[:, cols],
-                rhs=rc[:].bitcast(E4M3),
-                rhs_scale=rs[:],
-                start=start,
-                stop=stop,
+        def copy_out(engine, key, tile_index):
+            if key not in leaving:
+                if key[0] == "dx":
+                    leaving[key] = big_pool.tile([P, PACK, D_IN], F32, name="big", align_bytes=ALIGN)
+                else:
+                    leaving[key] = dw_pool.tile([P, PACK, D_IN], F32, name="dw", align_bytes=ALIGN)
+            copy(engine, leaving[key][:, tile_index, :], banks[key + (tile_index,)][:])
+
+
+        def quantize(key, part=0, parts=1):
+            e5m2 = key[0] in ("g", "token", "hidden")
+            if key not in codes:
+                pools = {"w2": w2_pool, "token": token_codes_pool, "hidden": hidden_codes_pool}
+                shared = key[0] in pools and key[1] != "x"
+                pool = pools[key[0]] if shared else keep
+                tag = key[0] if shared else "_".join([str(v) for v in key])
+                words = pool.tile([P, SPAN], U32, name="words_" + tag, align_bytes=ALIGN)
+                scales = pool.tile([P, SPAN], U8, name="scales_" + tag, align_bytes=ALIGN)
+                codes[key] = (words, scales)
+            words, scales = codes[key]
+            width = SPAN // parts
+            cols = slice(part * width, (part + 1) * width)
+            nc.vector.quantize_mx(
+                out=words[:, cols].bitcast(E5M2 if e5m2 else E4M3),
+                scales=scales[:, cols],
+                in_=packed[key][:].rearrange("p c k -> p (c k)")[:, PACK * cols.start : PACK * cols.stop],
             )
 
-        def dc(grp, h, t):
-            bank = ps_mm.tile([P, W], F32, name="mm")
-            for pas in range(N_P):
-                mx(bank, ("g", grp, pas), t, ("w2", h, pas), pas == 0, pas == N_P - 1)
-            banks["dc", grp, h, t] = bank
+        def quantize_g(group, pair):
+            for i in range(PASSES):
+                quantize(("g", group, i), pair, 2)
 
-        def mask(grp, h, t):
-            if ("dz", grp, h) not in groups:
-                groups["dz", grp, h] = dz_pool.tile([P, PACK, W], BF16, name="dz", align_bytes=64)
-            dz = groups["dz", grp, h]
-            bank = banks["dc", grp, h, t]
-            zv = raws["z", grp, h][:, t, :].rearrange("p (q u e) -> p u q e", u=2, e=2)
+        def mask(group, chunk, pair):
+            if (group, chunk) not in masked:
+                masked[group, chunk] = dz_pool.tile([P, PACK, SPAN], BF16, name="dz", align_bytes=ALIGN)
+            for j in (2 * pair, 2 * pair + 1):
+                z_sorted = loaded["z", group, chunk, pair][:, j % 2, :].rearrange("p (q u e) -> p u q e", u=2, e=2)
+                for u in range(2):
+                    half = slice(u * SPAN // 2, (u + 1) * SPAN // 2)
+                    nc.vector.scalar_tensor_tensor(
+                        out=masked[group, chunk][:, j, half].rearrange("p (q e) -> p q e", e=2),
+                        in0=z_sorted[:, u],
+                        scalar=0.0,
+                        in1=banks["dc", group, chunk, j][:, half].rearrange("p (q e) -> p q e", e=2),
+                        op0=mybir.AluOpType.is_gt,
+                        op1=mybir.AluOpType.mult,
+                    )
+
+
+        def turn(key, pair, words, starts, step):
+            bank = turns.tile([P, 2, 2 * P], F32, name="turn")
             for u in range(2):
-                half = slice(u * 256, (u + 1) * 256)
-                nc.vector.scalar_tensor_tensor(
-                    out=dz[:, t, half].rearrange("p (q e) -> p q e", e=2),
-                    in0=zv[:, u],
-                    scalar=0.0,
-                    in1=bank[:, half].rearrange("p (q e) -> p q e", e=2),
-                    op0=IS_GT,
-                    op1=MULT,
+                for t in range(2):
+                    first = starts[t] + u * (1 if step == 2 else P)
+                    nc.tensor.transpose(
+                        bank[:, u, t * P : (t + 1) * P], words[:, first : first + step * (P - 1) + 1 : step], identity[:]
+                    )
+            banks[key + (pair,)] = bank
+
+        def turn_g(group, pair):
+            words = loaded[group][:].rearrange("p j o -> p (j o)").bitcast(F32)
+            for i in range(PASSES):
+                turn(("g", group, i), pair, words, [(j * OUT + i * SPAN) // 2 for j in (2 * pair, 2 * pair + 1)], 2)
+
+        def turn_dz(group, chunk):
+            words = masked[group, chunk][:].rearrange("p j f -> p (j f)").bitcast(F32)
+            for pair in range(2):
+                turn(("hidden", group, chunk), pair, words, [j * SPAN // 2 for j in (2 * pair, 2 * pair + 1)], 1)
+
+        def multiply(key, terms, columns, which):
+            cols = slice(columns * P, (columns + 1) * P)
+            for i in which:
+                if i == 0:
+                    banks[key] = sums.tile([P, SPAN], F32, name="sum")
+                (left, left_scales), (right, right_scales) = codes[terms[i][0]], codes[terms[i][1]]
+                nc.tensor.matmul_mx(
+                    out=banks[key][:],
+                    lhsT=left[:, cols].bitcast(E5M2),
+                    lhsT_scale=left_scales[:, cols],
+                    rhs=right[:].bitcast(E4M3),
+                    rhs_scale=right_scales[:],
+                    start=i == 0,
+                    stop=i == len(terms) - 1,
                 )
 
-        def int_a(grp, h):
-            ga = grpa_pool.tile([P, W, PACK], BF16, name="ga", align_bytes=64)
-            dst = ga[:].rearrange("p (u e q i) t -> p u q t i e", u=2, e=2, i=2)
-            src = groups["dz", grp, h][:].rearrange("p t (u q i e) -> p u q t i e", u=2, e=2, i=2)
-            for u in range(2):
-                nc.vector.tensor_copy(out=dst[:, u], in_=src[:, u])
-            groups["a", grp, h] = ga
+        def dc(group, chunk, pair):
+            terms = [(("g", group, i), ("w2", chunk, i)) for i in range(PASSES)]
+            for j in (2 * pair, 2 * pair + 1):
+                multiply(("dc", group, chunk, j), terms, j, range(PASSES))
 
-        outs = {}
+        def dw(chunk, pair):
+            terms = [(("token", group, chunk), ("x", group)) for group in range(GROUPS)]
+            for c in (2 * pair, 2 * pair + 1):
+                multiply(("dw", chunk, c), terms, c, range(GROUPS))
 
-        def product_term(key, terms, t, i):
-            if i == 0:
-                banks[key] = ps_mm.tile([P, W], F32, name="mm")
-            mx(banks[key], terms[i][0], t, terms[i][1], i == 0, i == len(terms) - 1)
-
-        def out_tile(key):
-            if key not in outs:
-                outs[key] = (out_pool.tile([P, PACK, D_IN], F32, name="o1", align_bytes=64) if key[0] == "o1" else graw_pool.tile([P, PACK, D_IN], F32, name="graw", align_bytes=64))
-            return outs[key]
-
-        def evac(key, t, engine):
-            copy(engine, out_tile(key[:2])[:, t, :], banks[key][:])
-
-        def evac_add(key, t):
-            o = out_tile(key[:2])[:, t, :]
-            nc.vector.tensor_tensor(out=o, in0=banks[key][:], in1=o, op=ADD)
-
-        def store(key, t, n):
-            rows = out1_rows if key[0] == "o1" else out0_rows
-            nc.sync.dma_start(out=rows[key[1], :, t : t + n, :], in_=outs[key][:, t : t + n, :])
-
-        def out0_terms(grp, parts):
-            r = []
-            for part in parts:
-                if part == "x":
-                    r.extend([(("g", grp, pas), ("w2x", pas)) for pas in range(N_P)])
-                else:
-                    r.append((("b", grp, part), ("w1", part)))
-            return r
+        def dx(group, pair, part):
+            terms = [(("g", group, i), ("w2", "x", i)) for i in range(PASSES)]
+            terms += [(("hidden", group, h), ("w1", h)) for h in range(CHUNKS)]
+            for j in (2 * pair, 2 * pair + 1):
+                multiply(("dx", group, j), terms, j, range(PASSES) if part == "x" else [PASSES + part])
 
 
-        MODES = {(grp, t): [["x", 0, 1, 2, 3]] for grp in range(2) for t in range(4)}
-        units = [(k % 2, k // 2) for k in range(2 * N_H)]
+        def store(key, first, n):
+            rows = dx_rows if key[0] == "dx" else dw_rows
+            nc.sync.dma_start(out=rows[key[1], :, first : first + n, :], in_=leaving[key][:, first : first + n, :])
 
-        def L(what, needs=()):
-            if what[0] == "g":
-                put("load", ("raw",) + what, needs, load_g, what[1], what[2])
-            elif what[0] == "z":
-                put("load", ("raw",) + what, needs, load_z, what[1], what[2])
+
+        steps = {}
+
+        def step(name, needs, function, *args):
+            steps[name] = (needs, function, args)
+
+        operands = [("w2", h, i) for h in list(range(CHUNKS)) + ["x"] for i in range(PASSES)]
+        operands += [("w1", h) for h in range(CHUNKS)] + [("x", group) for group in range(GROUPS)]
+        for key in operands:
+            name = ".".join([str(v) for v in key])
+            step("load." + name, [], load_operand, key)
+            step("pack." + name, ["load." + name], pack_operand, key)
+            step("q." + name, ["pack." + name], quantize, key)
+
+        for group in range(GROUPS):
+            for pair in range(2):
+                at = f".{group}.{pair}"
+                step("load.g" + at, [], load_g, group, pair)
+                step("turn.g" + at, ["load.g" + at], turn_g, group, pair)
+                step("copy.g" + at, ["turn.g" + at], copy_g, group, pair)
+                step("q.g" + at, ["copy.g" + at], quantize_g, group, pair)
+
+            for h in range(CHUNKS):
+                unit = f".{group}.{h}"
+                for pair in range(2):
+                    at = f"{unit}.{pair}"
+                    step("load.z" + at, [], load_z, group, h, pair)
+                    step("dc" + at, [f"q.g.{group}.{pair}", f"q.w2.{h}.0", f"q.w2.{h}.1"], dc, group, h, pair)
+                    step("mask" + at, ["dc" + at, "load.z" + at], mask, group, h, pair)
+                both = [f"mask{unit}.0", f"mask{unit}.1"]
+                step("pack.token" + unit, both, pack_by_token, group, h)
+                step("q.token" + unit, ["pack.token" + unit], quantize, ("token", group, h))
+                step("turn.dz" + unit, both, turn_dz, group, h)
+                step("copy.dz" + unit, ["turn.dz" + unit], copy_dz, group, h)
+                step("q.hidden" + unit, ["copy.dz" + unit], quantize, ("hidden", group, h))
+
+            for pair in range(2):
+                last = f"dx.{group}.{pair}.x"
+                step(last, [f"q.g.{group}.{pair}", "q.w2.x.0", "q.w2.x.1"], dx, group, pair, "x")
+                for h in range(CHUNKS):
+                    name = f"dx.{group}.{pair}.{h}"
+                    step(name, [last, f"q.hidden.{group}.{h}", f"q.w1.{h}"], dx, group, pair, h)
+                    last = name
+                for j in (2 * pair, 2 * pair + 1):
+                    step(f"out.dx.{group}.{j}", [last], copy_out, ("dx", group), j)
+                    step(f"store.dx.{group}.{j}", [f"out.dx.{group}.{j}"], store, ("dx", group), j, 1)
+
+        for h in range(CHUNKS):
+            for pair in range(2):
+                ready = [f"q.token.{group}.{h}" for group in range(GROUPS)] + [f"q.x.{group}" for group in range(GROUPS)]
+                step(f"dw.{h}.{pair}", ready, dw, h, pair)
+                for c in (2 * pair, 2 * pair + 1):
+                    step(f"out.dw.{h}.{c}", [f"dw.{h}.{pair}"], copy_out, ("dw", h), c)
+                step(f"store.dw.{h}.{pair}", [f"out.dw.{h}.{c}" for c in (2 * pair, 2 * pair + 1)], store, ("dw", h), 2 * pair, 2)
+
+        waiting = {engine: " ".join(rows).split() for engine, rows in QUEUES.items()}
+        written = set()
+        while any([len(queue) > 0 for queue in waiting.values()]):
+            free = [e for e in waiting if waiting[e] and all([need in written for need in steps[waiting[e][0]][0]])]
+            name = waiting[free[0]].pop(0)
+            function, args = steps[name][1:]
+            if name.split(".")[0] in ("pack", "copy", "out") and not name.startswith("pack.token"):
+                function(free[0], *args)
             else:
-                put("load", ("raw",) + what, needs, load_w, what)
-
-        def loaded_as(what):
-            return what
-
-        def V_int(what):
-            put("v", ("int",) + what, [("raw",) + loaded_as(what)], interleave, what, "v")
-
-        def S_int(what):
-            put("s", ("int",) + what, [("raw",) + loaded_as(what)], interleave, what, "s")
-
-        def V_q(what):
-            put("v", ("q",) + what, [("int",) + what], quantize, what, E4M3)
-
-        def PE_g(grp, pas, jp):
-            put("pe", ("trg", grp, pas, jp), [("raw", "g", grp, jp)], g_transpose, grp, pas, jp)
-
-        def C_g(grp, pas, jp, e="s"):
-            put(e, ("cg", grp, pas, jp), [("trg", grp, pas, jp)], copy_transposed, ("g", grp, pas), jp, e)
-
-        def V_qg(grp, pas, jp):
-            put("v", ("q", "g", grp, pas, jp), [("cg", grp, pas, jp)], quantize, ("g", grp, pas), E5M2, jp, 2)
-
-        def PE_dc(k, t):
-            grp, h = units[k]
-            put("pe", ("dc", k, t), [("q", "g", grp, p, t // 2) for p in range(N_P)] + [("q", "w2", h, p) for p in range(N_P)], dc, grp, h, t)
-
-        def V_m(k, t):
-            put("v", ("m", k, t), [("dc", k, t), ("raw", "z") + units[k]], mask, units[k][0], units[k][1], t)
-
-        def PE_tr(k):
-            for jp in range(2):
-                put("pe", ("trb", k, jp), [("m", k, 2 * jp), ("m", k, 2 * jp + 1)], b_transpose, units[k][0], units[k][1], jp)
-
-        def C_b(k, e="s"):
-            for jp in range(2):
-                put(e, ("cb", k, jp), [("trb", k, jp)], copy_transposed, ("b",) + units[k], jp, e)
-
-        def V_qB(k):
-            put("v", ("q", "b") + units[k], [("cb", k, 0), ("cb", k, 1)], quantize, ("b",) + units[k], E5M2)
-
-        def V_intA(k):
-            put("v", ("ia", k), [("m", k, t) for t in range(4)], int_a, units[k][0], units[k][1])
-
-        def V_qA(k):
-            put("v", ("q", "a") + units[k], [("ia", k)], quantize, ("a",) + units[k], E5M2)
-
-        def needs_of(terms):
-            r = []
-            for lhs, rhs in terms:
-                if lhs[0] == "g":
-                    r.extend([("q",) + lhs + (jp,) for jp in range(2)])
-                else:
-                    r.append(("q",) + lhs)
-                r.append(("q",) + rhs)
-            return r
-
-        def PE_job(key, terms, t, where):
-            for i in range(len(terms)):
-                n = ("pe",) + key + (() if i == len(terms) - 1 else ("term", i))
-                put("pe", n, needs_of(terms[i : i + 1]) + ([("pe",) + key + ("term", i - 1)] if i else []), product_term, key, terms, t, i)
-
-        def E_job(key, t, e):
-            put(e, ("ev",) + key[:2] + (t,), [("pe",) + key], evac, key, t, e)
-
-        def A_job(key, t):
-            put("v", ("ad",) + key[:2] + (t,), [("pe",) + key, ("ev",) + key[:2] + (t,)], evac_add, key, t)
-
-        def ST(key, t, n, kind):
-            put("store", ("st",) + key + (t,), [(kind,) + key + (i,) for i in range(t, t + n)], store, key, t, n)
-
-        def job(name, where, e):
-            if name[0] == "o1":
-                h, c = name[1:]
-                terms = [(("a", grp, h), ("x", grp)) for grp in range(N_G)]
-                PE_job(name, terms, c, where)
-                E_job(name, c, e)
-                if c % 2 == 1:
-                    ST(name[:2], c - 1, 2, "ev")
-            else:
-                grp, t, stage = name[1:]
-                stages = MODES[grp, t]
-                key = ("o0", grp, t, stage)
-                PE_job(key, out0_terms(grp, stages[stage]), t, where)
-                if stage == 0:
-                    E_job(("o0", grp, t, 0), t, e)
-                else:
-                    A_job(("o0", grp, t, stage), t)
-                if grp == 1 and stage == len(stages) - 1:
-                    ST(("o0", grp), t, 1, "ev" if stage == 0 else "ad")
-                elif stage == len(stages) - 1:
-                    ST(("o0", grp), t, 1, "ev" if stage == 0 else "ad")
-
-
-        seq = [("w2", 0, 0), ("g", 0, 0), ("w2", 0, 1), ("g", 0, 1), ("z", 0, 0), ("w2", 1, 0), ("g", 1, 0), ("g", 1, 1), ("z", 1, 0), ("w2", 1, 1), ("x", 0), ("x", 1), ("z", 0, 1),
-               ("w2", 2, 0), ("w2", 2, 1), ("z", 1, 1), ("w2x", 0), ("w2x", 1), ("w1", 0), ("w1", 1), ("z", 0, 2), ("z", 1, 2), ("w2", 3, 0), ("w2", 3, 1), ("z", 0, 3), ("w1", 2), ("w1", 3), ("z", 1, 3)]
-        for i, what in enumerate(seq):
-            need = [] if i < 13 else [("m", (i - 13) // 3, 1)]
-            L(what, need)
-
-        for jp in range(2):
-            for pas in range(N_P):
-                PE_g(0, pas, jp)
-                C_g(0, pas, jp)
-        V_int(("w2", 0, 0))
-        V_qg(0, 0, 0)
-        V_qg(0, 1, 0)
-        V_q(("w2", 0, 0))
-        V_int(("w2", 0, 1))
-        V_qg(0, 0, 1)
-        V_q(("w2", 0, 1))
-        V_qg(0, 1, 1)
-        PE_dc(0, 0)
-        PE_dc(0, 1)
-
-        steps = {
-            0: dict(v=[], s=[("w2", 1, 0)], j=[]),
-            1: dict(v=[("i", ("w2", 1, 1)), ("q", ("w2", 1, 0)), ("q", ("w2", 1, 1))], s=[("x", 0), ("x", 1)], j=[]),
-            2: dict(v=[("q", ("x", 0)), ("q", ("x", 1)), ("i", ("w2", 2, 0)), ("q", ("w2", 2, 0))], s=[("w2", 2, 1), ("w2x", 0)], j=[]),
-            3: dict(v=[("q", ("w2", 2, 1)), ("i", ("w2x", 1)), ("q", ("w2x", 0)), ("q", ("w2x", 1))], s=[("w1", 0), ("w1", 1)], j=[("o1", 0, c) for c in range(4)]),
-            4: dict(v=[("q", ("w1", 0)), ("q", ("w1", 1))], s=[("w2", 3, 0), ("w2", 3, 1)], j=[("o0", 0, t, 0) for t in range(3)]),
-            5: dict(v=[("q", ("w2", 3, 0)), ("q", ("w2", 3, 1))], s=[("w1", 2)], j=[("o0", 0, 3, 0)] + [("o1", 1, c) for c in range(4)]),
-            6: dict(v=[("q", ("w1", 2))], s=[("w1", 3)], j=[("o0", 1, t, 0) for t in range(4)]),
-            7: dict(v=[("q", ("w1", 3))], s=[], j=[("o1", 2, c) for c in range(4)] + [("o0", 0, t, len(MODES[0, t]) - 1) for t in range(0)]),
-        }
-        for k in range(len(units)):
-            todo = [j for j in steps[k]["j"] if not (j[0] == "o0" and len(MODES[j[1], j[2]]) == 1)]
-            vs = list(steps[k]["v"])
-            ss = list(steps[k]["s"])
-            if k > 0:
-                vs = vs[:1] + [("qa", k - 1)] + vs[1:2] + [("qb", k - 1)] + vs[2:]
-            nper = [len(vs) // 4 + (1 if i < len(vs) % 4 else 0) for i in range(4)]
-            early = len(todo) - 1 if len(todo) > 1 else 0
-            jper = [0] + [early // 3 + (1 if i >= 3 - early % 3 else 0) for i in range(3)]
-            for t in range(4):
-                V_m(k, t)
-                for i in range(nper[t]):
-                    it = vs.pop(0)
-                    if it[0] == "qb":
-                        V_qB(it[1])
-                    elif it[0] == "qa":
-                        V_qA(it[1])
-                    elif it[0] == "q":
-                        V_q(it[1])
-                    elif it[0] == "i":
-                        V_int(it[1])
-                    else:
-                        V_qg(it[1], 0, it[2])
-                        V_qg(it[1], 1, it[2])
-                if t < 2:
-                    PE_dc(k, t + 2)
-                if ss and t in (0, 2):
-                    S_int(ss.pop(0))
-                if k == 0 and t == 0:
-                    for jp in range(2):
-                        for pas in range(N_P):
-                            C_g(1, pas, jp)
-                if k == 0 and t == 1:
-                    for jp in range(2):
-                        for pas in range(N_P):
-                            PE_g(1, pas, jp)
-                for i in range(jper[t]):
-                    job(todo.pop(0), None, "s")
-            if k + 1 < len(units):
-                PE_dc(k + 1, 0)
-            PE_tr(k)
-            C_b(k)
-            for it in todo:
-                job(it, None, "s")
-            V_intA(k)
-            if k == 0:
-                for jp in range(2):
-                    for pas in range(N_P):
-                        V_qg(1, pas, jp)
-            if k + 1 < len(units):
-                PE_dc(k + 1, 1)
-        last = len(units) - 1
-        for t in range(4):
-            job(("o0", 0, t, len(MODES[0, t]) - 1), None, "v")
-            if t == 0:
-                V_qA(last)
-            if t == 1:
-                V_qB(last)
-        for c in range(4):
-            job(("o1", 3, c), None, "s")
-        for t in range(4):
-            job(("o0", 1, t, len(MODES[1, t]) - 1), None, "v")
-
-
-        by_name = {".".join([str(v) for v in op[0]]): (op[0], [] if op[0][0] == "raw" else op[1], op[2], op[3]) for q in queues.values() for op in q}
-        queues = {e: [by_name[n] for n in ORDERS[e].split()] for e in ORDERS}
-        done = set()
-        while any([len(q) > 0 for q in queues.values()]):
-            ready = [n for n in ("load", "v", "s", "pe") if queues[n] and all([need in done for need in queues[n][0][1]])]
-            assert ready, [(q[0][0], [n for n in q[0][1] if n not in done]) for q in queues.values() if q]
-            name, needs, fn, args = queues[ready[0]].pop(0)
-            now["engine"] = ready[0]
-            fn(*args)
-            done.add(name)
+                function(*args)
+            written.add(name)

@@ -25,38 +25,36 @@ ALIGN = 64
 
 QUEUES = {
     "sync": [
-        "load.g.0.0 load.g.0.1 load.w2.0.0 load.w2.1.0 load.w2.0.1 load.w2.1.1 load.z.0.0.0 load.x.1 load.z.0.0.1",
-        "load.x.0 load.g.1.0 load.g.1.1 load.z.0.1.0 load.z.0.1.1 load.w2.2.0 load.z.1.0.1 load.z.1.0.0",
-        "load.w2.3.1 load.z.1.1.1 load.w2.2.1 load.z.1.1.0 load.z.0.2.1 load.z.0.2.0 load.w2.3.0 load.z.1.2.0",
-        "load.z.1.2.1 load.z.0.3.1 load.z.0.3.0 load.w2.x.0 load.z.1.3.0 load.w2.x.1 load.w1.0 load.z.1.3.1",
-        "store.dw.1.0 store.dw.1.1 load.w1.1 load.w1.2 load.w1.3 store.dw.0.1 store.dw.0.0 store.dw.2.0",
-        "store.dw.2.1 store.dx.0.0 store.dx.0.1 store.dx.1.0 store.dx.1.3 store.dx.1.1 store.dx.1.2 store.dw.3.0",
-        "store.dw.3.1 store.dx.0.2 store.dx.0.3",
+        "load.g.0.1 load.g.1.0 load.g.0.0 load.w2.0.0 load.w2.0.1 load.g.1.1 load.z.0.0.1 load.z.0.0.0",
+        "load.w2.1.0 load.z.1.0.0 load.z.1.0.1 load.w2.1.1 load.x load.z.0.1.1 load.z.0.1.0 load.z.1.1.0",
+        "load.z.1.1.1 load.w2.x store.dw.0.1 load.w1.0 store.dw.0.0 load.w1.1 store.dw.1.1 store.dw.1.0",
+        "store.dw.2.0 store.dw.2.1 store.dx.0.3 store.dx.0.2 store.dx.0.0 store.dw.3.0 store.dx.0.1 store.dw.3.1",
+        "store.dx.1.0 store.dx.1.1 store.dx.1.2 store.dx.1.3",
     ],
     "vector": [
-        "q.g.0.0 copy.g.0.1 q.g.0.1 pack.w2.1.0 q.w2.0.0 pack.w2.0.1 q.w2.0.1 q.w2.1.0 mask.0.0.0 q.w2.1.1",
-        "mask.0.0.1 pack.token.0.0 q.x.1 q.token.0.0 q.x.0 q.g.1.0 mask.0.1.0 mask.0.1.1 q.g.1.1 pack.token.0.1",
-        "mask.1.0.1 mask.1.0.0 q.token.0.1 pack.token.1.0 q.w2.2.0 q.token.1.0 mask.1.1.1 mask.1.1.0 q.w2.3.1",
-        "q.w2.2.1 pack.token.1.1 mask.0.2.1 q.token.1.1 mask.0.2.0 mask.1.2.0 pack.token.0.2 mask.1.2.1 q.w2.3.0",
-        "pack.token.1.2 mask.0.3.0 mask.0.3.1 q.hidden.1.0 q.token.1.2 q.token.0.2 mask.1.3.0 mask.1.3.1 q.w2.x.0",
-        "q.w2.x.1 q.hidden.1.1 q.hidden.0.1 q.w1.0 q.hidden.0.3 pack.w1.1 q.hidden.0.0 q.w1.1 q.hidden.1.2",
-        "q.hidden.0.2 q.w1.2 pack.token.0.3 q.w1.3 q.hidden.1.3 pack.token.1.3 q.token.0.3 q.token.1.3 out.dx.1.2",
-        "out.dw.3.2 out.dw.3.3 out.dx.0.3",
+        "copy.g.0.1 q.g.0.1 q.g.1.0 copy.g.0.0 q.g.0.0 pack.w2.0.0 q.w2.1.0 pack.w2.0.1 q.w2.0.1 q.w2.0.0",
+        "q.w2.1.1 q.g.1.1 mask.0.0.1 mask.0.1.1 mask.0.0.0 mask.0.1.0 pack.w2.3.0 q.token.0.0 q.w2.3.0",
+        "q.hidden.0.0 mask.1.1.0 mask.1.0.0 mask.1.1.1 mask.1.0.1 pack.w2.3.1 q.token.0.1 q.w2.3.1 pack.w2.2.1",
+        "q.w2.2.0 q.w2.2.1 q.token.1.0 mask.0.3.1 mask.0.2.1 q.x.0 mask.0.2.0 q.x.1 mask.0.3.0 pack.token.0.2",
+        "mask.1.3.0 q.token.1.1 q.token.0.2 mask.1.2.0 mask.1.2.1 pack.token.1.2 out.dw.1.0 q.token.1.2",
+        "mask.1.3.1 q.hidden.1.0 q.w2.x.0 q.w2.x.1 pack.w1.1 out.dw.2.2 out.dw.2.1 q.w1.1 q.w1.0 q.hidden.0.3",
+        "q.hidden.1.1 q.hidden.0.2 q.hidden.0.1 pack.w1.3 q.w1.2 q.w1.3 pack.token.1.3 q.token.0.3 q.token.1.3",
+        "copy.dz.1.2 out.dw.3.0 q.hidden.1.2 out.dw.3.2 out.dw.3.3 q.hidden.1.3 out.dx.1.0 out.dx.1.1 out.dx.1.3",
     ],
     "scalar": [
-        "copy.g.0.0 pack.w2.0.0 pack.w2.1.1 pack.x.1 pack.x.0 copy.g.1.0 copy.g.1.1 copy.dz.0.0 copy.dz.0.1",
-        "pack.w2.2.0 pack.w2.3.1 copy.dz.1.0 pack.w2.2.1 out.dw.0.0 out.dw.0.3 copy.dz.1.1 out.dw.0.2 out.dw.0.1",
-        "pack.w2.3.0 out.dw.1.1 out.dw.1.0 copy.dz.0.2 out.dw.1.2 out.dw.1.3 copy.dz.1.2 pack.w2.x.0 pack.w2.x.1",
-        "copy.dz.0.3 pack.w1.0 out.dw.2.1 out.dw.2.0 out.dw.2.2 out.dw.2.3 pack.w1.2 pack.w1.3 copy.dz.1.3",
-        "out.dx.0.0 out.dx.0.1 out.dx.1.0 out.dx.1.3 out.dx.1.1 out.dw.3.0 out.dw.3.1 out.dx.0.2",
+        "copy.g.1.0 pack.w2.1.0 pack.w2.1.1 copy.g.1.1 pack.token.0.0 copy.dz.0.0 pack.w2.2.0 pack.token.0.1",
+        "copy.dz.1.1 pack.token.1.0 copy.dz.0.1 pack.x.0 copy.dz.1.0 pack.x.1 pack.token.1.1 copy.dz.0.2",
+        "out.dw.0.1 out.dw.0.2 out.dw.0.0 out.dw.0.3 copy.dz.0.3 pack.w2.x.0 pack.w2.x.1 out.dw.1.2 out.dw.1.3",
+        "out.dw.1.1 pack.w1.0 out.dw.2.3 out.dw.2.0 pack.w1.2 copy.dz.1.3 pack.token.0.3 out.dx.0.3 out.dx.0.2",
+        "out.dx.0.0 out.dx.0.1 out.dw.3.1 out.dx.1.2",
     ],
     "tensor": [
-        "turn.g.0.0 turn.g.0.1 dc.0.0.0 dc.0.0.1 dc.0.1.0 dc.0.1.1 turn.g.1.0 turn.g.1.1 turn.dz.0.0 turn.dz.0.1",
-        "dc.1.0.1 dc.1.0.0 dc.1.1.1 turn.dz.1.0 dc.1.1.0 dw.0.0 dw.0.1 turn.dz.1.1 dc.0.2.1 dc.1.2.0 dc.0.2.0",
-        "dw.1.0 turn.dz.0.2 dc.1.2.1 dw.1.1 turn.dz.1.2 dc.0.3.0 dc.0.3.1 dc.1.3.0 turn.dz.0.3 dc.1.3.1 dw.2.1",
-        "dw.2.0 turn.dz.1.3 dx.0.0.x dx.1.1.x dx.1.0.x dx.1.1.0 dx.1.0.0 dx.0.0.0 dx.0.0.1 dx.1.0.1 dx.1.1.1",
-        "dx.1.0.2 dx.1.1.2 dx.0.0.2 dx.0.0.3 dx.1.0.3 dx.1.1.3 dx.0.1.x dw.3.0 dw.3.1 dx.0.1.0 dx.0.1.1 dx.0.1.2",
-        "dx.0.1.3",
+        "turn.g.0.1 turn.g.1.0 turn.g.0.0 turn.g.1.1 dc.0.0.1 dc.0.1.1 dc.0.0.0 dc.0.1.0 dc.1.1.1 turn.dz.0.0",
+        "dc.1.0.0 dc.1.1.0 dc.1.0.1 turn.dz.1.1 turn.dz.0.1 dc.0.3.1 turn.dz.1.0 dc.0.2.1 dc.0.2.0 dc.0.3.0",
+        "dc.1.3.0 turn.dz.0.2 dw.0.0 dw.0.1 turn.dz.0.3 dc.1.2.0 dc.1.2.1 dc.1.3.1 dw.1.0 dw.1.1 dw.2.0",
+        "turn.dz.1.3 dw.2.1 dx.0.0.x dx.1.0.x dx.0.1.x dx.0.1.0 dx.0.0.0 dx.1.0.0 dx.1.0.1 turn.dz.1.2 dx.0.1.1",
+        "dx.0.0.1 dx.0.1.2 dx.0.1.3 dx.0.0.2 dx.0.0.3 dw.3.0 dw.3.1 dx.1.1.x dx.1.0.2 dx.1.1.0 dx.1.0.3 dx.1.1.1",
+        "dx.1.1.2 dx.1.1.3",
     ],
 }
 
@@ -71,12 +69,12 @@ def tile_dpn_v_kernel(tc, x, W1, b1, W2, b2, z1, grad_out, out_0, out_1):
 
         keep = sbuf("keep", 1)
         big_pool = sbuf("big", 2)
-        raw_pool = sbuf("raw", 6)
-        z_pool = sbuf("z", 9)
+        raw_pool = sbuf("raw", 4)
+        z_pool = sbuf("z", 5)
         dz_pool = sbuf("dz", 3)
-        packed_pool = sbuf("packed", 5)
+        packed_pool = sbuf("packed", 4)
         by_token_pool = sbuf("by_token", 2)
-        turned_pool = sbuf("turned", 6)
+        turned_pool = sbuf("turned", 5)
         w2_pool = sbuf("w2_codes", 6)
         token_codes_pool = sbuf("token_codes", 5)
         hidden_codes_pool = sbuf("hidden_codes", 8)
@@ -91,9 +89,9 @@ def tile_dpn_v_kernel(tc, x, W1, b1, W2, b2, z1, grad_out, out_0, out_1):
 
         g_rows = grad_out.rearrange("(g p j) o -> g p j o", g=GROUPS, j=PACK)
         z_rows = z1.rearrange("(g p j) h -> g p j h", g=GROUPS, j=PACK)
-        x_rows = x.rearrange("(g p j) d -> g p j d", g=GROUPS, j=PACK)
+        x_rows = x.rearrange("(g p j) d -> p g j d", g=GROUPS, j=PACK)
         w2_rows = W2.rearrange("(i p j) c -> i p j c", i=PASSES, j=PACK)
-        w1_rows = W1.rearrange("(h p j) d -> h p j d", h=CHUNKS, j=PACK)
+        w1_rows = W1.rearrange("(h p j) d -> p h j d", h=CHUNKS, j=PACK)
         dx_rows = out_0.rearrange("(g p j) d -> g p j d", g=GROUPS, j=PACK)
         dw_rows = out_1.rearrange("(h q c) d -> h q c d", h=CHUNKS, c=PACK)
 
@@ -111,23 +109,29 @@ def tile_dpn_v_kernel(tc, x, W1, b1, W2, b2, z1, grad_out, out_0, out_1):
             rows = slice(2 * pair, 2 * pair + 2)
             nc.sync.dma_start(out=loaded[group][:, rows, :], in_=g_rows[group, :, rows, :])
 
-        def load_z(group, chunk, pair):
-            tile = z_pool.tile([P, 2, SPAN], F32, name="z", align_bytes=ALIGN)
+        def load_z(group, half, pair):
+            tile = z_pool.tile([P, 2, 2 * SPAN], F32, name="z", align_bytes=ALIGN)
             rows = slice(2 * pair, 2 * pair + 2)
-            nc.sync.dma_start(out=tile[:], in_=z_rows[group, :, rows, chunk * SPAN : (chunk + 1) * SPAN])
-            loaded["z", group, chunk, pair] = tile
+            nc.sync.dma_start(out=tile[:], in_=z_rows[group, :, rows, 2 * half * SPAN : 2 * (half + 1) * SPAN])
+            for chunk in (2 * half, 2 * half + 1):
+                loaded["z", group, chunk, pair] = tile[:, :, (chunk % 2) * SPAN : (chunk % 2 + 1) * SPAN]
 
-        def load_operand(key):
-            tile = raw_pool.tile([P, PACK, SPAN], BF16, name="raw", align_bytes=ALIGN)
-            if key[0] == "w2":
-                first = 0 if key[1] == "x" else D_IN + key[1] * SPAN
-                source = w2_rows[key[2], :, :, first : first + SPAN]
-            elif key[0] == "w1":
-                source = w1_rows[key[1]]
+        def load_w2(half, i):
+            tile = raw_pool.tile([P, PACK, 2 * SPAN], BF16, name="raw", align_bytes=ALIGN)
+            first = D_IN + 2 * half * SPAN
+            nc.sync.dma_start(out=tile[:], in_=w2_rows[i, :, :, first : first + 2 * SPAN])
+            for chunk in (2 * half, 2 * half + 1):
+                loaded["w2", chunk, i] = tile[:, :, (chunk % 2) * SPAN : (chunk % 2 + 1) * SPAN]
+
+        def load_two(keys, sources):
+            tile = raw_pool.tile([P, 2, PACK, SPAN], BF16, name="raw", align_bytes=ALIGN)
+            if len(sources) == 1:
+                nc.sync.dma_start(out=tile[:], in_=sources[0])
             else:
-                source = x_rows[key[1]]
-            nc.sync.dma_start(out=tile[:], in_=source)
-            loaded[key] = tile
+                for n in range(2):
+                    nc.sync.dma_start(out=tile[:, n], in_=sources[n])
+            for n in range(2):
+                loaded[keys[n]] = tile[:, n]
 
 
         def copy(engine, out, in_):
@@ -138,7 +142,7 @@ def tile_dpn_v_kernel(tc, x, W1, b1, W2, b2, z1, grad_out, out_0, out_1):
 
         def pack_operand(engine, key):
             tile = packed_pool.tile([P, SPAN, PACK], BF16, name="packed", align_bytes=ALIGN)
-            source = loaded[key][:]
+            source = loaded[key]
             if key[0] == "w2" and key[1] != "x":
                 copy(
                     engine,
@@ -287,12 +291,21 @@ def tile_dpn_v_kernel(tc, x, W1, b1, W2, b2, z1, grad_out, out_0, out_1):
         def step(name, needs, function, *args):
             steps[name] = (needs, function, args)
 
-        operands = [("w2", h, i) for h in list(range(CHUNKS)) + ["x"] for i in range(PASSES)]
-        operands += [("w1", h) for h in range(CHUNKS)] + [("x", group) for group in range(GROUPS)]
-        for key in operands:
+        for half in range(CHUNKS // 2):
+            for i in range(PASSES):
+                step(f"load.w2.{half}.{i}", [], load_w2, half, i)
+            w1_pair = [("w1", 2 * half), ("w1", 2 * half + 1)]
+            step(f"load.w1.{half}", [], load_two, w1_pair, [w1_rows[:, 2 * half : 2 * half + 2]])
+        step("load.w2.x", [], load_two, [("w2", "x", i) for i in range(PASSES)], [w2_rows[i, :, :, 0:D_IN] for i in range(PASSES)])
+        step("load.x", [], load_two, [("x", group) for group in range(GROUPS)], [x_rows])
+
+        operands = [(("w2", h, i), f"load.w2.{h // 2}.{i}") for h in range(CHUNKS) for i in range(PASSES)]
+        operands += [(("w2", "x", i), "load.w2.x") for i in range(PASSES)]
+        operands += [(("w1", h), f"load.w1.{h // 2}") for h in range(CHUNKS)]
+        operands += [(("x", group), "load.x") for group in range(GROUPS)]
+        for key, load in operands:
             name = ".".join([str(v) for v in key])
-            step("load." + name, [], load_operand, key)
-            step("pack." + name, ["load." + name], pack_operand, key)
+            step("pack." + name, [load], pack_operand, key)
             step("q." + name, ["pack." + name], quantize, key)
 
         for group in range(GROUPS):
@@ -303,13 +316,16 @@ def tile_dpn_v_kernel(tc, x, W1, b1, W2, b2, z1, grad_out, out_0, out_1):
                 step("copy.g" + at, ["turn.g" + at], copy_g, group, pair)
                 step("q.g" + at, ["copy.g" + at], quantize_g, group, pair)
 
+            for half in range(CHUNKS // 2):
+                for pair in range(2):
+                    step(f"load.z.{group}.{half}.{pair}", [], load_z, group, half, pair)
+
             for h in range(CHUNKS):
                 unit = f".{group}.{h}"
                 for pair in range(2):
                     at = f"{unit}.{pair}"
-                    step("load.z" + at, [], load_z, group, h, pair)
                     step("dc" + at, [f"q.g.{group}.{pair}", f"q.w2.{h}.0", f"q.w2.{h}.1"], dc, group, h, pair)
-                    step("mask" + at, ["dc" + at, "load.z" + at], mask, group, h, pair)
+                    step("mask" + at, ["dc" + at, f"load.z.{group}.{h // 2}.{pair}"], mask, group, h, pair)
                 both = [f"mask{unit}.0", f"mask{unit}.1"]
                 step("pack.token" + unit, both, pack_by_token, group, h)
                 step("q.token" + unit, ["pack.token" + unit], quantize, ("token", group, h))

@@ -25,36 +25,45 @@ ALIGN = 64
 
 QUEUES = {
     "sync": [
-        "load.g.0.1 load.g.1.0 load.g.0.0 load.w2.0.0 load.w2.0.1 load.g.1.1 load.z.0.0.1 load.z.0.0.0",
-        "load.w2.1.0 load.z.1.0.0 load.z.1.0.1 load.w2.1.1 load.x load.z.0.1.1 load.z.0.1.0 load.z.1.1.0",
-        "load.z.1.1.1 load.w2.x store.dw.0.1 load.w1.0 store.dw.0.0 load.w1.1 store.dw.1.1 store.dw.1.0",
-        "store.dw.2.0 store.dw.2.1 store.dx.0.3 store.dx.0.2 store.dx.0.0 store.dw.3.0 store.dx.0.1 store.dw.3.1",
-        "store.dx.1.0 store.dx.1.1 store.dx.1.2 store.dx.1.3",
+        "load.g.0.0 load.g.1.0 load.w2.0.0 load.g.0.1 load.w2.0.1 load.w2.1.0 load.z.0.0.0 load.g.1.1",
+        "load.z.0.0.1 load.w2.1.1 load.z.1.0.0 load.z.1.0.1 load.x load.z.0.1.1 load.z.0.1.0 load.z.1.1.1",
+        "load.w2.x load.z.1.1.0 load.w1.0 load.w1.1 store.dw.0.1 store.dw.0.0 store.dw.1.1 store.dw.1.0",
+        "store.dx.0.0 store.dx.0.1 store.dx.0.2 store.dx.0.3 store.dw.2.0 store.dw.2.1 store.dx.1.3 store.dx.1.2",
+        "store.dx.1.1 store.dw.3.1 store.dw.3.0 store.dx.1.0",
     ],
     "vector": [
-        "copy.g.0.1 q.g.0.1 q.g.1.0 copy.g.0.0 q.g.0.0 pack.w2.0.0 q.w2.1.0 pack.w2.0.1 q.w2.0.1 q.w2.0.0",
-        "q.w2.1.1 q.g.1.1 mask.0.0.1 mask.0.1.1 mask.0.0.0 mask.0.1.0 pack.w2.3.0 q.token.0.0 q.w2.3.0",
-        "q.hidden.0.0 mask.1.1.0 mask.1.0.0 mask.1.1.1 mask.1.0.1 pack.w2.3.1 q.token.0.1 q.w2.3.1 pack.w2.2.1",
-        "q.w2.2.0 q.w2.2.1 q.token.1.0 mask.0.3.1 mask.0.2.1 q.x.0 mask.0.2.0 q.x.1 mask.0.3.0 pack.token.0.2",
-        "mask.1.3.0 q.token.1.1 q.token.0.2 mask.1.2.0 mask.1.2.1 pack.token.1.2 out.dw.1.0 q.token.1.2",
-        "mask.1.3.1 q.hidden.1.0 q.w2.x.0 q.w2.x.1 pack.w1.1 out.dw.2.2 out.dw.2.1 q.w1.1 q.w1.0 q.hidden.0.3",
-        "q.hidden.1.1 q.hidden.0.2 q.hidden.0.1 pack.w1.3 q.w1.2 q.w1.3 pack.token.1.3 q.token.0.3 q.token.1.3",
-        "copy.dz.1.2 out.dw.3.0 q.hidden.1.2 out.dw.3.2 out.dw.3.3 q.hidden.1.3 out.dx.1.0 out.dx.1.1 out.dx.1.3",
+        "q.g.0.0 copy.g.1.0 q.g.1.0 pack.w2.0.0.0 q.w2.0.0.0 q.w2.0.1.0 pack.w2.0.0.1 q.w2.0.0.1 q.g.0.1",
+        "q.w2.0.1.1 pack.w2.1.0.0 q.w2.1.0.0 mask.0.0.1.0 mask.0.0.0.0 mask.0.0.0.1 mask.0.0.1.1 q.w2.1.1.0",
+        "mask.0.0.0.3 mask.0.0.0.2 mask.0.0.1.2 q.g.1.1 mask.0.0.1.3 pack.w2.1.1.1 q.w2.1.1.1 q.token.0.0",
+        "mask.1.0.0.1 mask.1.0.0.0 mask.1.0.1.1 mask.1.0.1.0 mask.1.0.0.3 mask.1.0.0.2 q.w2.1.0.1 mask.1.0.1.2",
+        "mask.1.0.1.3 q.token.0.1 pack.x.1 mask.0.1.1.3 mask.0.1.0.3 mask.0.1.1.2 mask.0.1.0.2 copy.dz.1.1.1",
+        "mask.0.1.0.1 mask.0.1.0.0 mask.0.1.1.1 mask.0.1.1.0 q.token.1.0 q.x.1 q.x.0 mask.1.1.1.3 mask.1.1.0.2",
+        "mask.1.1.0.3 mask.1.1.1.2 q.hidden.0.0 q.token.1.1 mask.1.1.1.0 mask.1.1.0.1 mask.1.1.0.0 out.dw.0.3",
+        "q.w2.x.0 q.w2.x.1 mask.1.1.1.1 pack.w1.0 q.hidden.1.0 q.w1.0 q.hidden.0.2 q.hidden.0.1 pack.w1.3",
+        "pack.w1.2 q.w1.1 q.w1.3 q.w1.2 q.hidden.0.3 pack.token.0.2 q.hidden.1.1 q.token.0.2 q.token.1.2",
+        "pack.token.1.3 q.hidden.1.3 q.hidden.1.2 pack.token.0.3 q.token.1.3 q.token.0.3 out.dw.3.3 out.dw.3.1",
     ],
     "scalar": [
-        "copy.g.1.0 pack.w2.1.0 pack.w2.1.1 copy.g.1.1 pack.token.0.0 copy.dz.0.0 pack.w2.2.0 pack.token.0.1",
-        "copy.dz.1.1 pack.token.1.0 copy.dz.0.1 pack.x.0 copy.dz.1.0 pack.x.1 pack.token.1.1 copy.dz.0.2",
-        "out.dw.0.1 out.dw.0.2 out.dw.0.0 out.dw.0.3 copy.dz.0.3 pack.w2.x.0 pack.w2.x.1 out.dw.1.2 out.dw.1.3",
-        "out.dw.1.1 pack.w1.0 out.dw.2.3 out.dw.2.0 pack.w1.2 copy.dz.1.3 pack.token.0.3 out.dx.0.3 out.dx.0.2",
-        "out.dx.0.0 out.dx.0.1 out.dw.3.1 out.dx.1.2",
+        "copy.g.0.0 pack.w2.0.1.0 copy.g.0.1 pack.w2.0.1.1 pack.w2.1.1.0 copy.g.1.1 copy.dz.0.0.0 copy.dz.0.1.0",
+        "pack.token.0.0 copy.dz.0.0.1 copy.dz.0.1.1 pack.w2.1.0.1 pack.token.0.1 copy.dz.1.0.0 copy.dz.1.1.0",
+        "pack.token.1.0 copy.dz.1.0.1 pack.x.0 pack.token.1.1 copy.dz.0.2.1 pack.w2.x.0 out.dw.0.0 copy.dz.0.2.0",
+        "pack.w2.x.1 out.dw.0.2 out.dw.0.1 copy.dz.0.3.0 copy.dz.0.3.1 out.dw.1.1 out.dw.1.2 out.dw.1.3",
+        "copy.dz.1.2.1 out.dw.1.0 pack.w1.1 copy.dz.1.3.1 pack.token.1.2 copy.dz.1.2.0 copy.dz.1.3.0 out.dx.0.1",
+        "out.dx.0.0 out.dx.0.3 out.dx.0.2 out.dw.2.0 out.dw.2.1 out.dw.2.2 out.dw.2.3 out.dx.1.1 out.dx.1.3",
+        "out.dx.1.2 out.dw.3.2 out.dw.3.0 out.dx.1.0",
     ],
     "tensor": [
-        "turn.g.0.1 turn.g.1.0 turn.g.0.0 turn.g.1.1 dc.0.0.1 dc.0.1.1 dc.0.0.0 dc.0.1.0 dc.1.1.1 turn.dz.0.0",
-        "dc.1.0.0 dc.1.1.0 dc.1.0.1 turn.dz.1.1 turn.dz.0.1 dc.0.3.1 turn.dz.1.0 dc.0.2.1 dc.0.2.0 dc.0.3.0",
-        "dc.1.3.0 turn.dz.0.2 dw.0.0 dw.0.1 turn.dz.0.3 dc.1.2.0 dc.1.2.1 dc.1.3.1 dw.1.0 dw.1.1 dw.2.0",
-        "turn.dz.1.3 dw.2.1 dx.0.0.x dx.1.0.x dx.0.1.x dx.0.1.0 dx.0.0.0 dx.1.0.0 dx.1.0.1 turn.dz.1.2 dx.0.1.1",
-        "dx.0.0.1 dx.0.1.2 dx.0.1.3 dx.0.0.2 dx.0.0.3 dw.3.0 dw.3.1 dx.1.1.x dx.1.0.2 dx.1.1.0 dx.1.0.3 dx.1.1.1",
-        "dx.1.1.2 dx.1.1.3",
+        "turn.g.0.0 turn.g.1.0 turn.g.0.1 dc.0.0.0.0 dc.0.0.0.1 dc.0.0.1.0 dc.0.0.0.3 dc.0.0.1.2 dc.0.0.1.1",
+        "turn.g.1.1 dc.0.0.0.2 turn.dz.0.0.0 turn.dz.0.1.0 dc.0.0.1.3 dc.1.0.0.1 dc.1.0.0.0 turn.dz.0.0.1",
+        "turn.dz.0.1.1 dc.1.0.0.2 dc.1.0.1.0 dc.1.0.1.1 dc.1.0.0.3 dc.1.0.1.3 dc.1.0.1.2 dc.0.1.1.3 turn.dz.1.1.0",
+        "turn.dz.1.0.0 dc.0.1.1.2 dc.1.1.0.3 dc.0.1.0.3 dc.0.1.0.1 turn.dz.1.1.1 turn.dz.1.0.1 dc.0.1.0.2",
+        "dc.0.1.1.0 dc.0.1.0.0 dc.0.1.1.1 turn.dz.0.3.1 turn.dz.0.2.1 dc.1.1.0.2 dc.1.1.1.0 dc.1.1.0.1 dc.1.1.1.3",
+        "dc.1.1.1.2 turn.dz.0.2.0 dw.0.0 dw.0.3 dc.1.1.1.1 dw.0.2 dc.1.1.0.0 turn.dz.0.3.0 dw.0.1 dw.1.0 dw.1.2",
+        "dw.1.3 dw.1.1 dx.0.0.x turn.dz.1.3.1 turn.dz.1.2.1 dx.0.2.x dx.1.2.x dx.1.1.x dx.1.2.0 dx.0.3.x dx.1.1.0",
+        "dx.0.3.0 dx.0.1.x dx.0.0.0 dx.0.1.0 dx.0.2.0 turn.dz.1.2.0 turn.dz.1.3.0 dx.0.3.1 dx.0.1.1 dx.0.2.1",
+        "dx.0.0.1 dx.0.1.2 dx.0.2.2 dx.0.1.3 dx.0.0.2 dx.0.0.3 dx.0.3.2 dx.0.3.3 dx.0.2.3 dx.1.1.1 dx.1.3.x",
+        "dw.2.0 dw.2.1 dx.1.2.1 dw.2.2 dx.1.3.0 dw.2.3 dx.1.1.2 dx.1.3.1 dx.1.1.3 dx.1.3.2 dx.1.3.3 dx.1.2.2",
+        "dx.1.2.3 dw.3.2 dw.3.3 dw.3.1 dw.3.0 dx.1.0.x dx.1.0.0 dx.1.0.1 dx.1.0.2 dx.1.0.3",
     ],
 }
 
@@ -71,11 +80,11 @@ def tile_dpn_v_kernel(tc, x, W1, b1, W2, b2, z1, grad_out, out_0, out_1):
         big_pool = sbuf("big", 2)
         raw_pool = sbuf("raw", 4)
         z_pool = sbuf("z", 5)
-        dz_pool = sbuf("dz", 3)
+        dz_pool = sbuf("dz", 2)
         packed_pool = sbuf("packed", 4)
         by_token_pool = sbuf("by_token", 2)
         turned_pool = sbuf("turned", 5)
-        w2_pool = sbuf("w2_codes", 6)
+        weights_pool = sbuf("weights_codes", 9)
         token_codes_pool = sbuf("token_codes", 5)
         hidden_codes_pool = sbuf("hidden_codes", 8)
         dw_pool = sbuf("dw", 2)
@@ -113,15 +122,14 @@ def tile_dpn_v_kernel(tc, x, W1, b1, W2, b2, z1, grad_out, out_0, out_1):
             tile = z_pool.tile([P, 2, 2 * SPAN], F32, name="z", align_bytes=ALIGN)
             rows = slice(2 * pair, 2 * pair + 2)
             nc.sync.dma_start(out=tile[:], in_=z_rows[group, :, rows, 2 * half * SPAN : 2 * (half + 1) * SPAN])
-            for chunk in (2 * half, 2 * half + 1):
-                loaded["z", group, chunk, pair] = tile[:, :, (chunk % 2) * SPAN : (chunk % 2 + 1) * SPAN]
+            loaded["z", group, half, pair] = tile
 
         def load_w2(half, i):
             tile = raw_pool.tile([P, PACK, 2 * SPAN], BF16, name="raw", align_bytes=ALIGN)
             first = D_IN + 2 * half * SPAN
             nc.sync.dma_start(out=tile[:], in_=w2_rows[i, :, :, first : first + 2 * SPAN])
-            for chunk in (2 * half, 2 * half + 1):
-                loaded["w2", chunk, i] = tile[:, :, (chunk % 2) * SPAN : (chunk % 2 + 1) * SPAN]
+            for u in range(2):
+                loaded["w2", half, u, i] = tile[:].rearrange("p j (q u e) -> p u q j e", u=2, e=2)[:, u]
 
         def load_two(keys, sources):
             tile = raw_pool.tile([P, 2, PACK, SPAN], BF16, name="raw", align_bytes=ALIGN)
@@ -144,11 +152,7 @@ def tile_dpn_v_kernel(tc, x, W1, b1, W2, b2, z1, grad_out, out_0, out_1):
             tile = packed_pool.tile([P, SPAN, PACK], BF16, name="packed", align_bytes=ALIGN)
             source = loaded[key]
             if key[0] == "w2" and key[1] != "x":
-                copy(
-                    engine,
-                    tile[:].rearrange("p (u q e) j -> p q j u e", u=2, e=2),
-                    source.rearrange("p j (q u e) -> p q j u e", u=2, e=2),
-                )
+                copy(engine, tile[:].rearrange("p (q e) j -> p q j e", e=2), source)
             else:
                 copy(
                     engine,
@@ -157,12 +161,12 @@ def tile_dpn_v_kernel(tc, x, W1, b1, W2, b2, z1, grad_out, out_0, out_1):
                 )
             packed[key] = tile
 
-        def pack_by_token(group, chunk):
+        def pack_by_token(engine, group, chunk):
             tile = by_token_pool.tile([P, SPAN, PACK], BF16, name="by_token", align_bytes=ALIGN)
             out = tile[:].rearrange("p (u e q i) j -> p u q j i e", u=2, e=2, i=2)
-            source = masked[group, chunk][:].rearrange("p j (u q i e) -> p u q j i e", u=2, i=2, e=2)
+            source = masked[group, chunk // 2][:].rearrange("p j (u c q i e) -> p u c q j i e", u=2, c=2, i=2, e=2)[:, :, chunk % 2]
             for u in range(2):
-                nc.vector.tensor_copy(out=out[:, u], in_=source[:, u])
+                copy(engine, out[:, u], source[:, u])
             packed["token", group, chunk] = tile
 
         def copy_turned(engine, key, pair):
@@ -174,10 +178,6 @@ def tile_dpn_v_kernel(tc, x, W1, b1, W2, b2, z1, grad_out, out_0, out_1):
         def copy_g(engine, group, pair):
             for i in range(PASSES):
                 copy_turned(engine, ("g", group, i), pair)
-
-        def copy_dz(engine, group, chunk):
-            for pair in range(2):
-                copy_turned(engine, ("hidden", group, chunk), pair)
 
         def copy_out(engine, key, tile_index):
             if key not in leaving:
@@ -191,10 +191,10 @@ def tile_dpn_v_kernel(tc, x, W1, b1, W2, b2, z1, grad_out, out_0, out_1):
         def quantize(key, part=0, parts=1):
             e5m2 = key[0] in ("g", "token", "hidden")
             if key not in codes:
-                pools = {"w2": w2_pool, "token": token_codes_pool, "hidden": hidden_codes_pool}
-                shared = key[0] in pools and key[1] != "x"
+                pools = {"w2": weights_pool, "w1": weights_pool, "token": token_codes_pool, "hidden": hidden_codes_pool}
+                shared = key[0] in pools
                 pool = pools[key[0]] if shared else keep
-                tag = key[0] if shared else "_".join([str(v) for v in key])
+                tag = {"w1": "weights", "w2": "weights"}.get(key[0], key[0]) if shared else "_".join([str(v) for v in key])
                 words = pool.tile([P, SPAN], U32, name="words_" + tag, align_bytes=ALIGN)
                 scales = pool.tile([P, SPAN], U8, name="scales_" + tag, align_bytes=ALIGN)
                 codes[key] = (words, scales)
@@ -211,28 +211,24 @@ def tile_dpn_v_kernel(tc, x, W1, b1, W2, b2, z1, grad_out, out_0, out_1):
             for i in range(PASSES):
                 quantize(("g", group, i), pair, 2)
 
-        def mask(group, chunk, pair):
-            if (group, chunk) not in masked:
-                masked[group, chunk] = dz_pool.tile([P, PACK, SPAN], BF16, name="dz", align_bytes=ALIGN)
-            for j in (2 * pair, 2 * pair + 1):
-                z_sorted = loaded["z", group, chunk, pair][:, j % 2, :].rearrange("p (q u e) -> p u q e", u=2, e=2)
-                for u in range(2):
-                    half = slice(u * SPAN // 2, (u + 1) * SPAN // 2)
-                    nc.vector.scalar_tensor_tensor(
-                        out=masked[group, chunk][:, j, half].rearrange("p (q e) -> p q e", e=2),
-                        in0=z_sorted[:, u],
-                        scalar=0.0,
-                        in1=banks["dc", group, chunk, j][:, half].rearrange("p (q e) -> p q e", e=2),
-                        op0=mybir.AluOpType.is_gt,
-                        op1=mybir.AluOpType.mult,
-                    )
+        def mask(group, half, u, j):
+            if (group, half) not in masked:
+                masked[group, half] = dz_pool.tile([P, PACK, 2 * SPAN], BF16, name="dz", align_bytes=ALIGN)
+            nc.vector.scalar_tensor_tensor(
+                out=masked[group, half][:, j, u * SPAN : (u + 1) * SPAN].rearrange("p (q e) -> p q e", e=2),
+                in0=loaded["z", group, half, j // 2][:, j % 2, :].rearrange("p (q u e) -> p u q e", u=2, e=2)[:, u],
+                scalar=0.0,
+                in1=banks["dc", group, half, u, j][:].rearrange("p (q e) -> p q e", e=2),
+                op0=mybir.AluOpType.is_gt,
+                op1=mybir.AluOpType.mult,
+            )
 
 
         def turn(key, pair, words, starts, step):
             bank = turns.tile([P, 2, 2 * P], F32, name="turn")
             for u in range(2):
                 for t in range(2):
-                    first = starts[t] + u * (1 if step == 2 else P)
+                    first = starts[t] + u * (1 if step == 2 else SPAN // 2)
                     nc.tensor.transpose(
                         bank[:, u, t * P : (t + 1) * P], words[:, first : first + step * (P - 1) + 1 : step], identity[:]
                     )
@@ -243,10 +239,9 @@ def tile_dpn_v_kernel(tc, x, W1, b1, W2, b2, z1, grad_out, out_0, out_1):
             for i in range(PASSES):
                 turn(("g", group, i), pair, words, [(j * OUT + i * SPAN) // 2 for j in (2 * pair, 2 * pair + 1)], 2)
 
-        def turn_dz(group, chunk):
-            words = masked[group, chunk][:].rearrange("p j f -> p (j f)").bitcast(F32)
-            for pair in range(2):
-                turn(("hidden", group, chunk), pair, words, [j * SPAN // 2 for j in (2 * pair, 2 * pair + 1)], 1)
+        def turn_dz(group, chunk, pair):
+            words = masked[group, chunk // 2][:].rearrange("p j f -> p (j f)").bitcast(F32)
+            turn(("hidden", group, chunk), pair, words, [j * SPAN + (chunk % 2) * P for j in (2 * pair, 2 * pair + 1)], 1)
 
         def multiply(key, terms, columns, which):
             cols = slice(columns * P, (columns + 1) * P)
@@ -264,21 +259,18 @@ def tile_dpn_v_kernel(tc, x, W1, b1, W2, b2, z1, grad_out, out_0, out_1):
                     stop=i == len(terms) - 1,
                 )
 
-        def dc(group, chunk, pair):
-            terms = [(("g", group, i), ("w2", chunk, i)) for i in range(PASSES)]
-            for j in (2 * pair, 2 * pair + 1):
-                multiply(("dc", group, chunk, j), terms, j, range(PASSES))
+        def dc(group, half, u, j):
+            terms = [(("g", group, i), ("w2", half, u, i)) for i in range(PASSES)]
+            multiply(("dc", group, half, u, j), terms, j, range(PASSES))
 
-        def dw(chunk, pair):
+        def dw(chunk, c):
             terms = [(("token", group, chunk), ("x", group)) for group in range(GROUPS)]
-            for c in (2 * pair, 2 * pair + 1):
-                multiply(("dw", chunk, c), terms, c, range(GROUPS))
+            multiply(("dw", chunk, c), terms, c, range(GROUPS))
 
-        def dx(group, pair, part):
+        def dx(group, j, part):
             terms = [(("g", group, i), ("w2", "x", i)) for i in range(PASSES)]
             terms += [(("hidden", group, h), ("w1", h)) for h in range(CHUNKS)]
-            for j in (2 * pair, 2 * pair + 1):
-                multiply(("dx", group, j), terms, j, range(PASSES) if part == "x" else [PASSES + part])
+            multiply(("dx", group, j), terms, j, range(PASSES) if part == "x" else [PASSES + part])
 
 
         def store(key, first, n):
@@ -299,7 +291,7 @@ def tile_dpn_v_kernel(tc, x, W1, b1, W2, b2, z1, grad_out, out_0, out_1):
         step("load.w2.x", [], load_two, [("w2", "x", i) for i in range(PASSES)], [w2_rows[i, :, :, 0:D_IN] for i in range(PASSES)])
         step("load.x", [], load_two, [("x", group) for group in range(GROUPS)], [x_rows])
 
-        operands = [(("w2", h, i), f"load.w2.{h // 2}.{i}") for h in range(CHUNKS) for i in range(PASSES)]
+        operands = [(("w2", half, u, i), f"load.w2.{half}.{i}") for half in range(CHUNKS // 2) for u in range(2) for i in range(PASSES)]
         operands += [(("w2", "x", i), "load.w2.x") for i in range(PASSES)]
         operands += [(("w1", h), f"load.w1.{h // 2}") for h in range(CHUNKS)]
         operands += [(("x", group), "load.x") for group in range(GROUPS)]
@@ -320,36 +312,40 @@ def tile_dpn_v_kernel(tc, x, W1, b1, W2, b2, z1, grad_out, out_0, out_1):
                 for pair in range(2):
                     step(f"load.z.{group}.{half}.{pair}", [], load_z, group, half, pair)
 
+            for half in range(CHUNKS // 2):
+                for u in range(2):
+                    for j in range(PACK):
+                        at = f".{group}.{half}.{u}.{j}"
+                        codes_needed = [f"q.g.{group}.{j // 2}"] + [f"q.w2.{half}.{u}.{i}" for i in range(PASSES)]
+                        step("dc" + at, codes_needed, dc, group, half, u, j)
+                        step("mask" + at, ["dc" + at, f"load.z.{group}.{half}.{j // 2}"], mask, group, half, u, j)
+
             for h in range(CHUNKS):
                 unit = f".{group}.{h}"
-                for pair in range(2):
-                    at = f"{unit}.{pair}"
-                    step("dc" + at, [f"q.g.{group}.{pair}", f"q.w2.{h}.0", f"q.w2.{h}.1"], dc, group, h, pair)
-                    step("mask" + at, ["dc" + at, f"load.z.{group}.{h // 2}.{pair}"], mask, group, h, pair)
-                both = [f"mask{unit}.0", f"mask{unit}.1"]
-                step("pack.token" + unit, both, pack_by_token, group, h)
+                masked_first = [[f"mask.{group}.{h // 2}.{u}.{j}" for u in range(2)] for j in range(PACK)]
+                step("pack.token" + unit, [n for row in masked_first for n in row], pack_by_token, group, h)
                 step("q.token" + unit, ["pack.token" + unit], quantize, ("token", group, h))
-                step("turn.dz" + unit, both, turn_dz, group, h)
-                step("copy.dz" + unit, ["turn.dz" + unit], copy_dz, group, h)
-                step("q.hidden" + unit, ["copy.dz" + unit], quantize, ("hidden", group, h))
+                for pair in range(2):
+                    step(f"turn.dz{unit}.{pair}", masked_first[2 * pair] + masked_first[2 * pair + 1], turn_dz, group, h, pair)
+                    step(f"copy.dz{unit}.{pair}", [f"turn.dz{unit}.{pair}"], copy_turned, ("hidden", group, h), pair)
+                step("q.hidden" + unit, [f"copy.dz{unit}.{pair}" for pair in range(2)], quantize, ("hidden", group, h))
 
-            for pair in range(2):
-                last = f"dx.{group}.{pair}.x"
-                step(last, [f"q.g.{group}.{pair}", "q.w2.x.0", "q.w2.x.1"], dx, group, pair, "x")
+            for j in range(PACK):
+                last = f"dx.{group}.{j}.x"
+                step(last, [f"q.g.{group}.{j // 2}", "q.w2.x.0", "q.w2.x.1"], dx, group, j, "x")
                 for h in range(CHUNKS):
-                    name = f"dx.{group}.{pair}.{h}"
-                    step(name, [last, f"q.hidden.{group}.{h}", f"q.w1.{h}"], dx, group, pair, h)
-                    last = name
-                for j in (2 * pair, 2 * pair + 1):
-                    step(f"out.dx.{group}.{j}", [last], copy_out, ("dx", group), j)
-                    step(f"store.dx.{group}.{j}", [f"out.dx.{group}.{j}"], store, ("dx", group), j, 1)
+                    part = f"dx.{group}.{j}.{h}"
+                    step(part, [last, f"q.hidden.{group}.{h}", f"q.w1.{h}"], dx, group, j, h)
+                    last = part
+                step(f"out.dx.{group}.{j}", [last], copy_out, ("dx", group), j)
+                step(f"store.dx.{group}.{j}", [f"out.dx.{group}.{j}"], store, ("dx", group), j, 1)
 
         for h in range(CHUNKS):
             for pair in range(2):
                 ready = [f"q.token.{group}.{h}" for group in range(GROUPS)] + [f"q.x.{group}" for group in range(GROUPS)]
-                step(f"dw.{h}.{pair}", ready, dw, h, pair)
                 for c in (2 * pair, 2 * pair + 1):
-                    step(f"out.dw.{h}.{c}", [f"dw.{h}.{pair}"], copy_out, ("dw", h), c)
+                    step(f"dw.{h}.{c}", ready, dw, h, c)
+                    step(f"out.dw.{h}.{c}", [f"dw.{h}.{c}"], copy_out, ("dw", h), c)
                 step(f"store.dw.{h}.{pair}", [f"out.dw.{h}.{c}" for c in (2 * pair, 2 * pair + 1)], store, ("dw", h), 2 * pair, 2)
 
         waiting = {engine: " ".join(rows).split() for engine, rows in QUEUES.items()}
@@ -358,7 +354,7 @@ def tile_dpn_v_kernel(tc, x, W1, b1, W2, b2, z1, grad_out, out_0, out_1):
             free = [e for e in waiting if waiting[e] and all([need in written for need in steps[waiting[e][0]][0]])]
             name = waiting[free[0]].pop(0)
             function, args = steps[name][1:]
-            if name.split(".")[0] in ("pack", "copy", "out") and not name.startswith("pack.token"):
+            if name.split(".")[0] in ("pack", "copy", "out"):
                 function(free[0], *args)
             else:
                 function(*args)

from contextlib import ExitStack

import concourse.mybir as mybir
from concourse.masks import make_identity

B, D_IN, HID, OUT = 1024, 512, 2048, 1024

FLOPS = 2 * B * OUT * (D_IN + HID) + 2 * (2 * B * HID * D_IN)
BYTES = 2 * (B * D_IN + HID * D_IN + OUT * (D_IN + HID) + B * OUT) + 4 * B * HID + 4 * (B * D_IN + HID * D_IN)

F32 = mybir.dt.float32
BF16 = mybir.dt.bfloat16
U32 = mybir.dt.uint32
U8 = mybir.dt.uint8
E4M3 = mybir.dt.float8_e4m3fn_x4
E5M2 = mybir.dt.float8_e5m2_x4

P = 128
PACK = 4
SPAN = P * PACK
GROUPS = B // SPAN
CHUNKS = HID // SPAN
PASSES = OUT // SPAN
ALIGN = 64

QUEUES = {
    "sync": [
        "load.g.0.0 load.g.1.0 load.w2.0.0 load.g.0.1 load.w2.0.1 load.w2.1.0 load.z.0.0.0 load.g.1.1",
        "load.z.0.0.1 load.w2.1.1 load.z.1.0.0 load.z.1.0.1 load.x load.z.0.1.1 load.z.0.1.0 load.z.1.1.1",
        "load.w2.x load.z.1.1.0 load.w1.0 load.w1.1 store.dw.0.1 store.dw.0.0 store.dw.1.1 store.dw.1.0",
        "store.dx.0.0 store.dx.0.1 store.dx.0.2 store.dx.0.3 store.dw.2.0 store.dw.2.1 store.dx.1.3 store.dx.1.2",
        "store.dx.1.1 store.dw.3.1 store.dw.3.0 store.dx.1.0",
    ],
    "vector": [
        "q.g.0.0 copy.g.1.0 q.g.1.0 pack.w2.0.0.0 q.w2.0.0.0 q.w2.0.1.0 pack.w2.0.0.1 q.w2.0.0.1 q.g.0.1",
        "q.w2.0.1.1 pack.w2.1.0.0 q.w2.1.0.0 mask.0.0.1.0 mask.0.0.0.0 mask.0.0.0.1 mask.0.0.1.1 q.w2.1.1.0",
        "mask.0.0.0.3 mask.0.0.0.2 mask.0.0.1.2 q.g.1.1 mask.0.0.1.3 pack.w2.1.1.1 q.w2.1.1.1 q.token.0.0",
        "mask.1.0.0.1 mask.1.0.0.0 mask.1.0.1.1 mask.1.0.1.0 mask.1.0.0.3 mask.1.0.0.2 q.w2.1.0.1 mask.1.0.1.2",
        "mask.1.0.1.3 q.token.0.1 pack.x.1 mask.0.1.1.3 mask.0.1.0.3 mask.0.1.1.2 mask.0.1.0.2 copy.dz.1.1.1",
        "mask.0.1.0.1 mask.0.1.0.0 mask.0.1.1.1 mask.0.1.1.0 q.token.1.0 q.x.1 q.x.0 mask.1.1.1.3 mask.1.1.0.2",
        "mask.1.1.0.3 mask.1.1.1.2 q.hidden.0.0 q.token.1.1 mask.1.1.1.0 mask.1.1.0.1 mask.1.1.0.0 out.dw.0.3",
        "q.w2.x.0 q.w2.x.1 mask.1.1.1.1 pack.w1.0 q.hidden.1.0 q.w1.0 q.hidden.0.2 q.hidden.0.1 pack.w1.3",
        "pack.w1.2 q.w1.1 q.w1.3 q.w1.2 q.hidden.0.3 pack.token.0.2 q.hidden.1.1 q.token.0.2 q.token.1.2",
        "pack.token.1.3 q.hidden.1.3 q.hidden.1.2 pack.token.0.3 q.token.1.3 q.token.0.3 out.dw.3.3 out.dw.3.1",
    ],
    "scalar": [
        "copy.g.0.0 pack.w2.0.1.0 copy.g.0.1 pack.w2.0.1.1 pack.w2.1.1.0 copy.g.1.1 copy.dz.0.0.0 copy.dz.0.1.0",
        "pack.token.0.0 copy.dz.0.0.1 copy.dz.0.1.1 pack.w2.1.0.1 pack.token.0.1 copy.dz.1.0.0 copy.dz.1.1.0",
        "pack.token.1.0 copy.dz.1.0.1 pack.x.0 pack.token.1.1 copy.dz.0.2.1 pack.w2.x.0 out.dw.0.0 copy.dz.0.2.0",
        "pack.w2.x.1 out.dw.0.2 out.dw.0.1 copy.dz.0.3.0 copy.dz.0.3.1 out.dw.1.1 out.dw.1.2 out.dw.1.3",
        "copy.dz.1.2.1 out.dw.1.0 pack.w1.1 copy.dz.1.3.1 pack.token.1.2 copy.dz.1.2.0 copy.dz.1.3.0 out.dx.0.1",
        "out.dx.0.0 out.dx.0.3 out.dx.0.2 out.dw.2.0 out.dw.2.1 out.dw.2.2 out.dw.2.3 out.dx.1.1 out.dx.1.3",
        "out.dx.1.2 out.dw.3.2 out.dw.3.0 out.dx.1.0",
    ],
    "tensor": [
        "turn.g.0.0 turn.g.1.0 turn.g.0.1 dc.0.0.0.0 dc.0.0.0.1 dc.0.0.1.0 dc.0.0.0.3 dc.0.0.1.2 dc.0.0.1.1",
        "turn.g.1.1 dc.0.0.0.2 turn.dz.0.0.0 turn.dz.0.1.0 dc.0.0.1.3 dc.1.0.0.1 dc.1.0.0.0 turn.dz.0.0.1",
        "turn.dz.0.1.1 dc.1.0.0.2 dc.1.0.1.0 dc.1.0.1.1 dc.1.0.0.3 dc.1.0.1.3 dc.1.0.1.2 dc.0.1.1.3 turn.dz.1.1.0",
        "turn.dz.1.0.0 dc.0.1.1.2 dc.1.1.0.3 dc.0.1.0.3 dc.0.1.0.1 turn.dz.1.1.1 turn.dz.1.0.1 dc.0.1.0.2",
        "dc.0.1.1.0 dc.0.1.0.0 dc.0.1.1.1 turn.dz.0.3.1 turn.dz.0.2.1 dc.1.1.0.2 dc.1.1.1.0 dc.1.1.0.1 dc.1.1.1.3",
        "dc.1.1.1.2 turn.dz.0.2.0 dw.0.0 dw.0.3 dc.1.1.1.1 dw.0.2 dc.1.1.0.0 turn.dz.0.3.0 dw.0.1 dw.1.0 dw.1.2",
        "dw.1.3 dw.1.1 dx.0.0.x turn.dz.1.3.1 turn.dz.1.2.1 dx.0.2.x dx.1.2.x dx.1.1.x dx.1.2.0 dx.0.3.x dx.1.1.0",
        "dx.0.3.0 dx.0.1.x dx.0.0.0 dx.0.1.0 dx.0.2.0 turn.dz.1.2.0 turn.dz.1.3.0 dx.0.3.1 dx.0.1.1 dx.0.2.1",
        "dx.0.0.1 dx.0.1.2 dx.0.2.2 dx.0.1.3 dx.0.0.2 dx.0.0.3 dx.0.3.2 dx.0.3.3 dx.0.2.3 dx.1.1.1 dx.1.3.x",
        "dw.2.0 dw.2.1 dx.1.2.1 dw.2.2 dx.1.3.0 dw.2.3 dx.1.1.2 dx.1.3.1 dx.1.1.3 dx.1.3.2 dx.1.3.3 dx.1.2.2",
        "dx.1.2.3 dw.3.2 dw.3.3 dw.3.1 dw.3.0 dx.1.0.x dx.1.0.0 dx.1.0.1 dx.1.0.2 dx.1.0.3",
    ],
}


def tile_dpn_v_kernel(tc, x, W1, b1, W2, b2, z1, grad_out, out_0, out_1):
    nc = tc.nc

    with ExitStack() as ctx:

        def sbuf(name, bufs):
            return ctx.enter_context(tc.tile_pool(name=name, bufs=bufs))

        keep = sbuf("keep", 1)
        big_pool = sbuf("big", 2)
        raw_pool = sbuf("raw", 4)
        z_pool = sbuf("z", 5)
        dz_pool = sbuf("dz", 2)
        packed_pool = sbuf("packed", 4)
        by_token_pool = sbuf("by_token", 2)
        turned_pool = sbuf("turned", 5)
        weights_pool = sbuf("weights_codes", 9)
        token_codes_pool = sbuf("token_codes", 5)
        hidden_codes_pool = sbuf("hidden_codes", 8)
        dw_pool = sbuf("dw", 2)
        sums = ctx.enter_context(tc.psum_pool(name="sums", bufs=6))
        turns = ctx.enter_context(tc.psum_pool(name="turns", bufs=2))

        identity = keep.tile([P, P], F32, name="identity", align_bytes=ALIGN)
        make_identity(nc, identity[:])

        ctx.enter_context(tc.manual_schedule())

        g_rows = grad_out.rearrange("(g p j) o -> g p j o", g=GROUPS, j=PACK)
        z_rows = z1.rearrange("(g p j) h -> g p j h", g=GROUPS, j=PACK)
        x_rows = x.rearrange("(g p j) d -> p g j d", g=GROUPS, j=PACK)
        w2_rows = W2.rearrange("(i p j) c -> i p j c", i=PASSES, j=PACK)
        w1_rows = W1.rearrange("(h p j) d -> p h j d", h=CHUNKS, j=PACK)
        dx_rows = out_0.rearrange("(g p j) d -> g p j d", g=GROUPS, j=PACK)
        dw_rows = out_1.rearrange("(h q c) d -> h q c d", h=CHUNKS, c=PACK)

        loaded = {}
        packed = {}
        codes = {}
        masked = {}
        banks = {}
        leaving = {}


        def load_g(group, pair):
            if group not in loaded:
                loaded[group] = big_pool.tile([P, PACK, OUT], BF16, name="big", align_bytes=ALIGN)
            rows = slice(2 * pair, 2 * pair + 2)
            nc.sync.dma_start(out=loaded[group][:, rows, :], in_=g_rows[group, :, rows, :])

        def load_z(group, half, pair):
            tile = z_pool.tile([P, 2, 2 * SPAN], F32, name="z", align_bytes=ALIGN)
            rows = slice(2 * pair, 2 * pair + 2)
            nc.sync.dma_start(out=tile[:], in_=z_rows[group, :, rows, 2 * half * SPAN : 2 * (half + 1) * SPAN])
            loaded["z", group, half, pair] = tile

        def load_w2(half, i):
            tile = raw_pool.tile([P, PACK, 2 * SPAN], BF16, name="raw", align_bytes=ALIGN)
            first = D_IN + 2 * half * SPAN
            nc.sync.dma_start(out=tile[:], in_=w2_rows[i, :, :, first : first + 2 * SPAN])
            for u in range(2):
                loaded["w2", half, u, i] = tile[:].rearrange("p j (q u e) -> p u q j e", u=2, e=2)[:, u]

        def load_two(keys, sources):
            tile = raw_pool.tile([P, 2, PACK, SPAN], BF16, name="raw", align_bytes=ALIGN)
            if len(sources) == 1:
                nc.sync.dma_start(out=tile[:], in_=sources[0])
            else:
                for n in range(2):
                    nc.sync.dma_start(out=tile[:, n], in_=sources[n])
            for n in range(2):
                loaded[keys[n]] = tile[:, n]


        def copy(engine, out, in_):
            if engine == "scalar":
                nc.scalar.copy(out=out, in_=in_)
            else:
                nc.vector.tensor_copy(out=out, in_=in_)

        def pack_operand(engine, key):
            tile = packed_pool.tile([P, SPAN, PACK], BF16, name="packed", align_bytes=ALIGN)
            source = loaded[key]
            if key[0] == "w2" and key[1] != "x":
                copy(engine, tile[:].rearrange("p (q e) j -> p q j e", e=2), source)
            else:
                copy(
                    engine,
                    tile[:].rearrange("p (q i) j -> p q j i", i=4),
                    source.rearrange("p j (q i) -> p q j i", i=4),
                )
            packed[key] = tile

        def pack_by_token(engine, group, chunk):
            tile = by_token_pool.tile([P, SPAN, PACK], BF16, name="by_token", align_bytes=ALIGN)
            out = tile[:].rearrange("p (u e q i) j -> p u q j i e", u=2, e=2, i=2)
            source = masked[group, chunk // 2][:].rearrange("p j (u c q i e) -> p u c q j i e", u=2, c=2, i=2, e=2)[:, :, chunk % 2]
            for u in range(2):
                copy(engine, out[:, u], source[:, u])
            packed["token", group, chunk] = tile

        def copy_turned(engine, key, pair):
            if key not in packed:
                packed[key] = turned_pool.tile([P, SPAN, PACK], BF16, name="turned", align_bytes=ALIGN)
            words = packed[key][:].rearrange("p t k -> p (t k)").bitcast(F32)[:, pair * SPAN : (pair + 1) * SPAN]
            copy(engine, words.rearrange("p (t u) -> p t u", u=2), banks[key + (pair,)][:].rearrange("p u t -> p t u"))

        def copy_g(engine, group, pair):
            for i in range(PASSES):
                copy_turned(engine, ("g", group, i), pair)

        def copy_out(engine, key, tile_index):
            if key not in leaving:
                if key[0] == "dx":
                    leaving[key] = big_pool.tile([P, PACK, D_IN], F32, name="big", align_bytes=ALIGN)
                else:
                    leaving[key] = dw_pool.tile([P, PACK, D_IN], F32, name="dw", align_bytes=ALIGN)
            copy(engine, leaving[key][:, tile_index, :], banks[key + (tile_index,)][:])


        def quantize(key, part=0, parts=1):
            e5m2 = key[0] in ("g", "token", "hidden")
            if key not in codes:
                pools = {"w2": weights_pool, "w1": weights_pool, "token": token_codes_pool, "hidden": hidden_codes_pool}
                shared = key[0] in pools
                pool = pools[key[0]] if shared else keep
                tag = {"w1": "weights", "w2": "weights"}.get(key[0], key[0]) if shared else "_".join([str(v) for v in key])
                words = pool.tile([P, SPAN], U32, name="words_" + tag, align_bytes=ALIGN)
                scales = pool.tile([P, SPAN], U8, name="scales_" + tag, align_bytes=ALIGN)
                codes[key] = (words, scales)
            words, scales = codes[key]
            width = SPAN // parts
            cols = slice(part * width, (part + 1) * width)
            nc.vector.quantize_mx(
                out=words[:, cols].bitcast(E5M2 if e5m2 else E4M3),
                scales=scales[:, cols],
                in_=packed[key][:].rearrange("p c k -> p (c k)")[:, PACK * cols.start : PACK * cols.stop],
            )

        def quantize_g(group, pair):
            for i in range(PASSES):
                quantize(("g", group, i), pair, 2)

        def mask(group, half, u, j):
            if (group, half) not in masked:
                masked[group, half] = dz_pool.tile([P, PACK, 2 * SPAN], BF16, name="dz", align_bytes=ALIGN)
            nc.vector.scalar_tensor_tensor(
                out=masked[group, half][:, j, u * SPAN : (u + 1) * SPAN].rearrange("p (q e) -> p q e", e=2),
                in0=loaded["z", group, half, j // 2][:, j % 2, :].rearrange("p (q u e) -> p u q e", u=2, e=2)[:, u],
                scalar=0.0,
                in1=banks["dc", group, half, u, j][:].rearrange("p (q e) -> p q e", e=2),
                op0=mybir.AluOpType.is_gt,
                op1=mybir.AluOpType.mult,
            )


        def turn(key, pair, words, starts, step):
            bank = turns.tile([P, 2, 2 * P], F32, name="turn")
            for u in range(2):
                for t in range(2):
                    first = starts[t] + u * (1 if step == 2 else SPAN // 2)
                    nc.tensor.transpose(
                        bank[:, u, t * P : (t + 1) * P], words[:, first : first + step * (P - 1) + 1 : step], identity[:]
                    )
            banks[key + (pair,)] = bank

        def turn_g(group, pair):
            words = loaded[group][:].rearrange("p j o -> p (j o)").bitcast(F32)
            for i in range(PASSES):
                turn(("g", group, i), pair, words, [(j * OUT + i * SPAN) // 2 for j in (2 * pair, 2 * pair + 1)], 2)

        def turn_dz(group, chunk, pair):
            words = masked[group, chunk // 2][:].rearrange("p j f -> p (j f)").bitcast(F32)
            turn(("hidden", group, chunk), pair, words, [j * SPAN + (chunk % 2) * P for j in (2 * pair, 2 * pair + 1)], 1)

        def multiply(key, terms, columns, which):
            cols = slice(columns * P, (columns + 1) * P)
            for i in which:
                if i == 0:
                    banks[key] = sums.tile([P, SPAN], F32, name="sum")
                (left, left_scales), (right, right_scales) = codes[terms[i][0]], codes[terms[i][1]]
                nc.tensor.matmul_mx(
                    out=banks[key][:],
                    lhsT=left[:, cols].bitcast(E5M2),
                    lhsT_scale=left_scales[:, cols],
                    rhs=right[:].bitcast(E4M3),
                    rhs_scale=right_scales[:],
                    start=i == 0,
                    stop=i == len(terms) - 1,
                )

        def dc(group, half, u, j):
            terms = [(("g", group, i), ("w2", half, u, i)) for i in range(PASSES)]
            multiply(("dc", group, half, u, j), terms, j, range(PASSES))

        def dw(chunk, c):
            terms = [(("token", group, chunk), ("x", group)) for group in range(GROUPS)]
            multiply(("dw", chunk, c), terms, c, range(GROUPS))

        def dx(group, j, part):
            terms = [(("g", group, i), ("w2", "x", i)) for i in range(PASSES)]
            terms += [(("hidden", group, h), ("w1", h)) for h in range(CHUNKS)]
            multiply(("dx", group, j), terms, j, range(PASSES) if part == "x" else [PASSES + part])


        def store(key, first, n):
            rows = dx_rows if key[0] == "dx" else dw_rows
            nc.sync.dma_start(out=rows[key[1], :, first : first + n, :], in_=leaving[key][:, first : first + n, :])


        steps = {}

        def step(name, needs, function, *args):
            steps[name] = (needs, function, args)

        for half in range(CHUNKS // 2):
            for i in range(PASSES):
                step(f"load.w2.{half}.{i}", [], load_w2, half, i)
            w1_pair = [("w1", 2 * half), ("w1", 2 * half + 1)]
            step(f"load.w1.{half}", [], load_two, w1_pair, [w1_rows[:, 2 * half : 2 * half + 2]])
        step("load.w2.x", [], load_two, [("w2", "x", i) for i in range(PASSES)], [w2_rows[i, :, :, 0:D_IN] for i in range(PASSES)])
        step("load.x", [], load_two, [("x", group) for group in range(GROUPS)], [x_rows])

        operands = [(("w2", half, u, i), f"load.w2.{half}.{i}") for half in range(CHUNKS // 2) for u in range(2) for i in range(PASSES)]
        operands += [(("w2", "x", i), "load.w2.x") for i in range(PASSES)]
        operands += [(("w1", h), f"load.w1.{h // 2}") for h in range(CHUNKS)]
        operands += [(("x", group), "load.x") for group in range(GROUPS)]
        for key, load in operands:
            name = ".".join([str(v) for v in key])
            step("pack." + name, [load], pack_operand, key)
            step("q." + name, ["pack." + name], quantize, key)

        for group in range(GROUPS):
            for pair in range(2):
                at = f".{group}.{pair}"
                step("load.g" + at, [], load_g, group, pair)
                step("turn.g" + at, ["load.g" + at], turn_g, group, pair)
                step("copy.g" + at, ["turn.g" + at], copy_g, group, pair)
                step("q.g" + at, ["copy.g" + at], quantize_g, group, pair)

            for half in range(CHUNKS // 2):
                for pair in range(2):
                    step(f"load.z.{group}.{half}.{pair}", [], load_z, group, half, pair)

            for half in range(CHUNKS // 2):
                for u in range(2):
                    for j in range(PACK):
                        at = f".{group}.{half}.{u}.{j}"
                        codes_needed = [f"q.g.{group}.{j // 2}"] + [f"q.w2.{half}.{u}.{i}" for i in range(PASSES)]
                        step("dc" + at, codes_needed, dc, group, half, u, j)
                        step("mask" + at, ["dc" + at, f"load.z.{group}.{half}.{j // 2}"], mask, group, half, u, j)

            for h in range(CHUNKS):
                unit = f".{group}.{h}"
                masked_first = [[f"mask.{group}.{h // 2}.{u}.{j}" for u in range(2)] for j in range(PACK)]
                step("pack.token" + unit, [n for row in masked_first for n in row], pack_by_token, group, h)
                step("q.token" + unit, ["pack.token" + unit], quantize, ("token", group, h))
                for pair in range(2):
                    step(f"turn.dz{unit}.{pair}", masked_first[2 * pair] + masked_first[2 * pair + 1], turn_dz, group, h, pair)
                    step(f"copy.dz{unit}.{pair}", [f"turn.dz{unit}.{pair}"], copy_turned, ("hidden", group, h), pair)
                step("q.hidden" + unit, [f"copy.dz{unit}.{pair}" for pair in range(2)], quantize, ("hidden", group, h))

            for j in range(PACK):
                last = f"dx.{group}.{j}.x"
                step(last, [f"q.g.{group}.{j // 2}", "q.w2.x.0", "q.w2.x.1"], dx, group, j, "x")
                for h in range(CHUNKS):
                    part = f"dx.{group}.{j}.{h}"
                    step(part, [last, f"q.hidden.{group}.{h}", f"q.w1.{h}"], dx, group, j, h)
                    last = part
                step(f"out.dx.{group}.{j}", [last], copy_out, ("dx", group), j)
                step(f"store.dx.{group}.{j}", [f"out.dx.{group}.{j}"], store, ("dx", group), j, 1)

        for h in range(CHUNKS):
            for pair in range(2):
                ready = [f"q.token.{group}.{h}" for group in range(GROUPS)] + [f"q.x.{group}" for group in range(GROUPS)]
                for c in (2 * pair, 2 * pair + 1):
                    step(f"dw.{h}.{c}", ready, dw, h, c)
                    step(f"out.dw.{h}.{c}", [f"dw.{h}.{c}"], copy_out, ("dw", h), c)
                step(f"store.dw.{h}.{pair}", [f"out.dw.{h}.{c}" for c in (2 * pair, 2 * pair + 1)], store, ("dw", h), 2 * pair, 2)

        waiting = {engine: " ".join(rows).split() for engine, rows in QUEUES.items()}
        written = set()
        while any([len(queue) > 0 for queue in waiting.values()]):
            free = [e for e in waiting if waiting[e] and all([need in written for need in steps[waiting[e][0]][0]])]
            name = waiting[free[0]].pop(0)
            function, args = steps[name][1:]
            if name.split(".")[0] in ("pack", "copy", "out"):
                function(free[0], *args)
            else:
                function(*args)
            written.add(name)
